import numpy as np
import ml_dtypes


def mxq(x, axis, fmt="e4m3"):
    dtype, down = {"e4m3": (ml_dtypes.float8_e4m3fn, 7), "e5m2": (ml_dtypes.float8_e5m2, 14)}[fmt]
    v = np.moveaxis(np.asarray(x, np.float32).astype(ml_dtypes.bfloat16).astype(np.float64), axis, -1)
    blocks = v.reshape(v.shape[:-1] + (-1, 32))
    amax = np.abs(blocks).max(-1, keepdims=True)
    byte = np.maximum(np.where(amax > 0, np.frexp(amax)[1] - 1 + 127, 0) - down, 1)
    scale = np.exp2(byte - 127.0)
    codes = (blocks / scale).astype(np.float32).astype(dtype).astype(np.float64)
    return np.moveaxis((codes * scale).reshape(v.shape), -1, axis)


WIDE = False


def mx_kscale(k):
    if not WIDE:
        return np.ones(k)
    levels = np.array([10, -10, 5, -5, 0])
    a = np.random.permutation(np.resize(levels, k // 512 * 4)).reshape(k // 512, 4)
    idx = np.arange(k)
    return np.exp2(a[idx // 512, idx % 128 // 32])


BF16 = ml_dtypes.bfloat16


def bf(x):
    return np.asarray(x, np.float32).astype(BF16)


def f64(x):
    return np.asarray(x).astype(np.float64)


E2M1 = np.array([0.0, 0.5, 1.0, 1.5, 2.0, 3.0, 4.0, 6.0, -0.0, -0.5, -1.0, -1.5, -2.0, -3.0, -4.0, -6.0])


def pack_weight(w, fmt):
    k, n = w.shape
    w = f64(bf(w)).reshape(k // 32, 32, n)
    amax = np.abs(w).max(1)
    if fmt == "e4m3":
        byte = np.frexp(amax)[1] - 1 + 127 - 7
    else:
        mant, ex = np.frexp(amax / 6.0)
        byte = np.where(mant > 0.5, ex, ex - 1) + 127
    byte = np.clip(np.where(amax > 0, byte, 1), 1, 254)
    scaled = (w * np.exp2(127.0 - byte)[:, None, :]).reshape(k, n).astype(np.float32)
    by_word = np.ascontiguousarray(scaled.reshape(k // 512, 128, 4, n).transpose(0, 1, 3, 2))
    if fmt == "e4m3":
        words = by_word.astype(ml_dtypes.float8_e4m3fn).view(np.uint8)
    else:
        c = by_word.astype(ml_dtypes.float4_e2m1fn).view(np.uint8) & 0xF
        words = c[..., 0::2] | (c[..., 1::2] << 4)
    return np.ascontiguousarray(words), np.ascontiguousarray(byte.astype(np.uint8).reshape(k // 512, 16, n))


def unpack_weight(words, scales, fmt):
    g, p, n, _ = words.shape
    if fmt == "e4m3":
        vals = np.ascontiguousarray(words).view(ml_dtypes.float8_e4m3fn).astype(np.float64)
    else:
        nib = np.empty((g, p, n, 4), np.uint8)
        nib[..., 0::2] = words & 0xF
        nib[..., 1::2] = words >> 4
        vals = E2M1[nib]
    vals = vals * np.repeat(np.exp2(scales.astype(np.float64) - 127.0), 8, axis=1)[..., None]
    return vals.transpose(0, 1, 3, 2).reshape(g * 512, n)

def pack4(w):
    words, scales = pack_weight(w, "e2m1")
    return words.reshape(words.shape[0], 128, -1), scales


def unpack4(words, scales):
    return unpack_weight(words.reshape(words.shape[0], 128, -1, 2), scales, "e2m1")


B, K, L, D, H = 4, 8, 256, 1024, 128


def erf(v):
    c = np.clip(v, -6.0, 6.0)
    q = 2.0 * c * c
    term = c.copy()
    total = c.copy()
    for n in range(1, 120):
        term = term * q / (2.0 * n + 1.0)
        total = total + term
    return 2.0 / np.sqrt(np.pi) * np.exp(-c * c) * total


def gelu_erf(v):
    return 0.5 * v * (1.0 + erf(v / np.sqrt(2.0)))


def sigmoid(v):
    return 1.0 / (1.0 + np.exp(-v))


def setup_inputs():
    t = mx_kscale(2 * D)[D:]
    wf = np.random.standard_normal((2 * D, D)) / np.sqrt(2 * D)
    wf[D:] = wf[D:] / t[:, None]
    wf_words, wf_scales = pack4(wf)
    return {
        "orig_feat": bf(np.random.standard_normal((B, L, D))),
        "rag_feat": bf(np.random.standard_normal((B, K, L, D)) * t),
        "af": bf(np.random.uniform(0.01, 0.99, (B, L))),
        "h_af": bf(np.maximum(np.random.standard_normal((B, L, H)), 0.0) * np.random.uniform(0.0, 1.0, (B, L, 1))),
        "w2": bf(np.random.standard_normal((H, D)) * 2.0 / np.sqrt(H)),
        "b2": bf(-np.log(D / 2.0) + 0.3 * np.random.standard_normal(D)),
        "wf_words": wf_words,
        "wf_scales": wf_scales,
        "bias_f": bf(np.random.standard_normal(D) * 0.5),
        "ln_g": bf(1.0 + 0.2 * np.random.standard_normal(D)),
        "ln_b": bf(0.3 * np.random.standard_normal(D)),
    }


def reference(orig_feat, rag_feat, af, h_af, w2, b2, wf_words, wf_scales, bias_f, ln_g, ln_b):
    o, r, a = f64(orig_feat), f64(rag_feat), f64(af)
    af_weight = sigmoid(f64(h_af) @ f64(w2) + f64(b2))
    s = af_weight.sum(-1)
    pooled_ref = (0.7 * r.mean(axis=1) + 0.3 * r.max(axis=1)) * s[:, :, None]
    x = np.concatenate([o, pooled_ref], axis=-1)
    y = (mxq(x, 2, "e4m3") @ unpack4(wf_words, wf_scales)) + f64(bias_f)
    mu = y.mean(-1, keepdims=True)
    var = ((y - mu) ** 2).mean(-1, keepdims=True)
    yn = (y - mu) / np.sqrt(var + 1e-5) * f64(ln_g) + f64(ln_b)
    fused = gelu_erf(yn)
    return o + fused * np.sqrt(a * (1.0 - a))[..., None]

@@ -1,0 +1,226 @@
+from contextlib import ExitStack
+
+import concourse.mybir as mybir
+from concourse.masks import make_identity
+
+F32 = mybir.dt.float32
+BF16 = mybir.dt.bfloat16
+I32 = mybir.dt.int32
+U32 = mybir.dt.uint32
+U8 = mybir.dt.uint8
+FP8X4 = mybir.dt.float8_e4m3fn_x4
+FP4X4 = mybir.dt.float4_e2m1fn_x4
+ALU = mybir.AluOpType
+ACT = mybir.ActivationFunctionType
+
+P = 128
+B, REFS, L, D, H = 4, 8, 256, 1024, 128
+J = L // P
+TILES = B * J
+PACK = 4
+K_PASS = P * PACK
+PASSES = 2 * D // K_PASS
+HALF_PASSES = PASSES // 2
+N_TILE = 512
+N_HALVES = D // N_TILE
+LN_EPS = 1e-5
+MEAN_W, MAX_W = 0.7, 0.3
+
+FLOPS = 2 * B * L * (2 * D) * D + 2 * B * L * H * D
+
+
+def tile_rarevariantawarefusion_pa_kernel(
+    tc, orig_feat, rag_feat, af, h_af, w2, b2, wf_words, wf_scales, bias_f, ln_g, ln_b, out
+):
+    nc = tc.nc
+    with ExitStack() as ctx:
+        const = ctx.enter_context(tc.tile_pool(name="const", bufs=1))
+        origs = ctx.enter_context(tc.tile_pool(name="origs", bufs=B))
+        rags = ctx.enter_context(tc.tile_pool(name="rags", bufs=2))
+        trees = ctx.enter_context(tc.tile_pool(name="trees", bufs=1))
+        work = ctx.enter_context(tc.tile_pool(name="work", bufs=2))
+        psum = ctx.enter_context(tc.psum_pool(name="psum", bufs=4))
+
+        w_planes = const.tile([P, PASSES, D], U8, align_bytes=64)
+        nc.vector.memset(w_planes[:].bitcast(I32), 0)
+        scale_rows = wf_scales.bitcast(I32).rearrange("g (q r) n -> r q g n", r=4)
+        for r in range(4):
+            nc.sync.dma_start(out=w_planes[:].bitcast(I32)[r:P:32], in_=scale_rows[r])
+
+        haf = const.tile([P, B, J, H], BF16)
+        nc.sync.dma_start(
+            out=haf[:].rearrange("p b j h -> p b (j h)"), in_=h_af.rearrange("b (p j) h -> p b (j h)", j=J)
+        )
+        w2_sb = const.tile([P, D], BF16)
+        nc.sync.dma_start(out=w2_sb[:], in_=w2)
+        af_sb = const.tile([P, B, J], BF16)
+        nc.sync.dma_start(out=af_sb[:], in_=af.rearrange("b (p j) -> p b j", j=J))
+
+        b2_bc = const.tile([P, D], BF16)
+        nc.scalar.dma_start(out=b2_bc[:], in_=b2.partition_broadcast(P))
+        biasf_bc = const.tile([P, D], BF16)
+        nc.scalar.dma_start(out=biasf_bc[:], in_=bias_f.partition_broadcast(P))
+        lng_bc = const.tile([P, D], BF16)
+        nc.scalar.dma_start(out=lng_bc[:], in_=ln_g.partition_broadcast(P))
+        lnb_bc = const.tile([P, D], BF16)
+        nc.scalar.dma_start(out=lnb_bc[:], in_=ln_b.partition_broadcast(P))
+
+        ident_f32 = const.tile([P, P], F32)
+        make_identity(nc, ident_f32[:])
+        ident_bf = const.tile([P, P], BF16)
+        make_identity(nc, ident_bf[:])
+
+        orig_sb = []
+        rag_sb = []
+        w_words = const.tile([P, PASSES, 2 * D], U8, align_bytes=64)
+
+        def load_batch(b):
+            o_t = origs.tile([P, J, D], BF16, name="o_t")
+            nc.sync.dma_start(
+                out=o_t[:].rearrange("p j d -> p (j d)"), in_=orig_feat[b].rearrange("(p j) d -> p (j d)", j=J)
+            )
+            orig_sb.append(o_t)
+            r_t = rags.tile([P, REFS, J, D], BF16, name="r_t")
+            rows = rag_feat[b].rearrange("k (p j) d -> p k (j d)", j=J)
+            for k in range(0, REFS, 2):
+                nc.sync.dma_start(out=r_t[:, k : k + 2].rearrange("p k j d -> p k (j d)"), in_=rows[:, k : k + 2])
+            rag_sb.append(r_t)
+
+        load_batch(0)
+        nc.sync.dma_start(out=w_words[:].bitcast(I32), in_=wf_words.rearrange("g p n -> p g n").bitcast(I32))
+
+        hT_ps = psum.tile([P, TILES, P], BF16, tag="xt")
+        for t in range(TILES):
+            nc.tensor.transpose(hT_ps[:, t, :], haf[:, t // J, t % J, :], ident_bf[:])
+        hT = const.tile([P, TILES, P], BF16)
+        nc.vector.tensor_copy(out=hT[:], in_=hT_ps[:])
+        s_all = const.tile([P, TILES], F32)
+        for t in range(TILES):
+            logits = work.tile([P, D], F32, tag="y")
+            for n in range(N_HALVES):
+                cols = slice(n * N_TILE, (n + 1) * N_TILE)
+                z_ps = psum.tile([P, N_TILE], F32, tag="acc")
+                nc.tensor.matmul(z_ps[:], lhsT=hT[:, t, :], rhs=w2_sb[:, cols], start=True, stop=True)
+                nc.vector.tensor_tensor(out=logits[:, cols], in0=z_ps[:], in1=b2_bc[:, cols], op=ALU.add)
+            gates = work.tile([P, D], BF16, tag="gates")
+            nc.scalar.activation(out=gates[:], in_=logits[:], func=ACT.Sigmoid, accum_out=s_all[:, t : t + 1])
+        s_max = const.tile([P, TILES], F32)
+        nc.vector.tensor_scalar_mul(out=s_max[:], in0=s_all[:], scalar1=MAX_W)
+
+        half = const.tile([P, TILES], F32)
+        nc.vector.memset(half[:], 0.5)
+        neg_half = const.tile([P, 1], F32)
+        nc.vector.memset(neg_half[:], -0.5)
+        af_flat = af_sb[:].rearrange("p b j -> p (b j)")
+        one_minus = const.tile([P, TILES], F32)
+        nc.vector.tensor_scalar(out=one_minus[:], in0=af_flat, scalar1=-1.0, scalar2=1.0, op0=ALU.mult, op1=ALU.add)
+        spread = const.tile([P, TILES], F32)
+        nc.vector.tensor_tensor(out=spread[:], in0=one_minus[:], in1=af_flat, op=ALU.mult)
+        af_scale = const.tile([P, TILES], F32)
+        nc.gpsimd.tensor_tensor(out=af_scale[:], in0=spread[:], in1=half[:], op=ALU.pow)
+
+        for b in range(B):
+            if b + 1 < B:
+                load_batch(b + 1)
+            o_t = orig_sb[b]
+            r_t = rag_sb[b]
+
+            m4 = trees.tile([P, 4, J * D], BF16)
+            nc.vector.tensor_tensor(
+                out=m4[:],
+                in0=r_t[:, 0:4].rearrange("p k j d -> p k (j d)"),
+                in1=r_t[:, 4:8].rearrange("p k j d -> p k (j d)"),
+                op=ALU.max,
+            )
+            m2 = trees.tile([P, 2, J * D], BF16)
+            nc.vector.tensor_tensor(out=m2[:], in0=m4[:, 0:2], in1=m4[:, 2:4], op=ALU.max)
+            m1 = trees.tile([P, J * D], BF16)
+            nc.vector.tensor_tensor(out=m1[:], in0=m2[:, 0], in1=m2[:, 1], op=ALU.max)
+
+            flat = r_t[:].rearrange("p k j d -> p k (j d)")
+            sum_a = trees.tile([P, J * D], F32)
+            sum_b = trees.tile([P, J * D], F32)
+            nc.vector.tensor_tensor(out=sum_a[:], in0=flat[:, 0], in1=flat[:, 1], op=ALU.add)
+            nc.vector.tensor_tensor(out=sum_b[:], in0=flat[:, 4], in1=flat[:, 5], op=ALU.add)
+            for k in (2, 3):
+                nc.vector.tensor_tensor(out=sum_a[:], in0=sum_a[:], in1=flat[:, k], op=ALU.add)
+                nc.vector.tensor_tensor(out=sum_b[:], in0=sum_b[:], in1=flat[:, k + 4], op=ALU.add)
+            nc.vector.tensor_tensor(out=sum_a[:], in0=sum_a[:], in1=sum_b[:], op=ALU.add)
+            nc.vector.scalar_tensor_tensor(
+                out=sum_a[:], in0=sum_a[:], scalar=MEAN_W / REFS / MAX_W, in1=m1[:], op0=ALU.mult, op1=ALU.add
+            )
+
+            for j in range(J):
+                t = b * J + j
+                pooled = work.tile([P, D], BF16)
+                nc.scalar.activation(
+                    out=pooled[:], in_=sum_a[:, j * D : (j + 1) * D], func=ACT.Copy, scale=s_max[:, t : t + 1]
+                )
+
+                grouped = work.tile([P, PASSES, P, PACK], BF16, align_bytes=64)
+                o_words = o_t[:, j, :].bitcast(F32)
+                oT_ps = psum.tile([P, HALF_PASSES, 2, P], F32, tag="xt")
+                for g in range(HALF_PASSES):
+                    for u in range(2):
+                        nc.tensor.transpose(
+                            oT_ps[:, g, u, :], o_words[:, 256 * g + u : 256 * (g + 1) : 2], ident_f32[:]
+                        )
+                o_grouped = (
+                    grouped[:, 0:HALF_PASSES]
+                    .rearrange("p g r i -> p (g r i)")
+                    .bitcast(F32)
+                    .rearrange("p (g r u) -> p g r u", g=HALF_PASSES, u=2)
+                )
+                nc.scalar.copy(out=o_grouped, in_=oT_ps[:].rearrange("p g u r -> p g r u"))
+                pT_ps = psum.tile([P, HALF_PASSES, PACK, P], BF16, tag="xt")
+                for g in range(HALF_PASSES):
+                    for i in range(PACK):
+                        nc.tensor.transpose(
+                            pT_ps[:, g, i, :], pooled[:, K_PASS * g + i : K_PASS * (g + 1) : PACK], ident_bf[:]
+                        )
+                nc.scalar.copy(out=grouped[:, HALF_PASSES:PASSES], in_=pT_ps[:].rearrange("p g i r -> p g r i"))
+
+                x_codes = work.tile([P, PASSES * P], U32, align_bytes=64)
+                x_planes = work.tile([P, PASSES * P], U8, align_bytes=64)
+                nc.vector.quantize_mx(
+                    out=x_codes[:].bitcast(FP8X4),
+                    scales=x_planes[:],
+                    in_=grouped[:].rearrange("p g r i -> p (g r i)"),
+                )
+
+                y = work.tile([P, D], F32, tag="y")
+                stats = work.tile([P, N_HALVES, 6], F32)
+                for n in range(N_HALVES):
+                    cols = slice(n * N_TILE, (n + 1) * N_TILE)
+                    acc = psum.tile([P, N_TILE], F32, tag="acc")
+                    for g in range(PASSES):
+                        nc.tensor.matmul_mx(
+                            out=acc[:],
+                            lhsT=x_codes[:, g * P : (g + 1) * P].bitcast(FP8X4),
+                            lhsT_scale=x_planes[:, g * P : (g + 1) * P],
+                            rhs=w_words[:, g, 2 * n * N_TILE : 2 * (n + 1) * N_TILE].bitcast(FP4X4),
+                            rhs_scale=w_planes[:, g, cols],
+                            start=(g == 0),
+                            stop=(g == PASSES - 1),
+                        )
+                    nc.vector.tensor_tensor(out=y[:, cols], in0=acc[:], in1=biasf_bc[:, cols], op=ALU.add)
+                    nc.vector.bn_stats(out=stats[:, n, :], in_=y[:, cols])
+                mean_var = work.tile([P, 2], F32)
+                nc.vector.bn_aggr(out=mean_var[:], in_=stats[:].rearrange("p n s -> p (n s)"))
+                var_eps = work.tile([P, 1], F32)
+                nc.vector.tensor_scalar_add(out=var_eps[:], in0=mean_var[:, 1:2], scalar1=LN_EPS)
+                rstd = work.tile([P, 1], F32)
+                nc.gpsimd.tensor_tensor(out=rstd[:], in0=var_eps[:], in1=neg_half[:], op=ALU.pow)
+                nc.vector.scalar_tensor_tensor(
+                    out=y[:], in0=y[:], scalar=mean_var[:, 0:1], in1=lng_bc[:], op0=ALU.subtract, op1=ALU.mult
+                )
+                nc.vector.scalar_tensor_tensor(
+                    out=y[:], in0=y[:], scalar=rstd[:], in1=lnb_bc[:], op0=ALU.mult, op1=ALU.add
+                )
+                fused = work.tile([P, D], F32)
+                nc.scalar.activation(out=fused[:], in_=y[:], func=ACT.Gelu)
+                res = work.tile([P, D], F32)
+                nc.vector.scalar_tensor_tensor(
+                    out=res[:], in0=fused[:], scalar=af_scale[:, t : t + 1], in1=o_t[:, j, :], op0=ALU.mult, op1=ALU.add
+                )
+                nc.sync.dma_start(out=out[b].rearrange("(p j) d -> p j d", j=J)[:, j, :], in_=res[:])

@@ -25,6 +25,8 @@ N_TILE = 512
 N_HALVES = D // N_TILE
 LN_EPS = 1e-5
 MEAN_W, MAX_W = 0.7, 0.3
+TERMS = REFS + 1
+SCALAR_TERMS = 5
 
 FLOPS = 2 * B * L * (2 * D) * D + 2 * B * L * H * D
 
@@ -38,8 +40,9 @@ def tile_rarevariantawarefusion_pa_kernel(
         origs = ctx.enter_context(tc.tile_pool(name="origs", bufs=B))
         rags = ctx.enter_context(tc.tile_pool(name="rags", bufs=2))
         trees = ctx.enter_context(tc.tile_pool(name="trees", bufs=1))
+        terms = ctx.enter_context(tc.tile_pool(name="terms", bufs=2))
         work = ctx.enter_context(tc.tile_pool(name="work", bufs=2))
-        psum = ctx.enter_context(tc.psum_pool(name="psum", bufs=4))
+        psum = ctx.enter_context(tc.psum_pool(name="psum", bufs=2))
 
         w_planes = const.tile([P, PASSES, D], U8, align_bytes=64)
         nc.vector.memset(w_planes[:].bitcast(I32), 0)
@@ -89,7 +92,7 @@ def tile_rarevariantawarefusion_pa_kernel(
         load_batch(0)
         nc.sync.dma_start(out=w_words[:].bitcast(I32), in_=wf_words.rearrange("g p n -> p g n").bitcast(I32))
 
-        hT_ps = psum.tile([P, TILES, P], BF16, tag="xt")
+        hT_ps = psum.tile([P, TILES, P], BF16, tag="oT")
         for t in range(TILES):
             nc.tensor.transpose(hT_ps[:, t, :], haf[:, t // J, t % J, :], ident_bf[:])
         hT = const.tile([P, TILES, P], BF16)
@@ -106,6 +109,8 @@ def tile_rarevariantawarefusion_pa_kernel(
             nc.scalar.activation(out=gates[:], in_=logits[:], func=ACT.Sigmoid, accum_out=s_all[:, t : t + 1])
         s_max = const.tile([P, TILES], F32)
         nc.vector.tensor_scalar_mul(out=s_max[:], in0=s_all[:], scalar1=MAX_W)
+        s_mean = const.tile([P, TILES], F32)
+        nc.vector.tensor_scalar_mul(out=s_mean[:], in0=s_all[:], scalar1=MEAN_W / REFS)
 
         half = const.tile([P, TILES], F32)
         nc.vector.memset(half[:], 0.5)
@@ -132,34 +137,27 @@ def tile_rarevariantawarefusion_pa_kernel(
                 in1=r_t[:, 4:8].rearrange("p k j d -> p k (j d)"),
                 op=ALU.max,
             )
-            m2 = trees.tile([P, 2, J * D], BF16)
-            nc.vector.tensor_tensor(out=m2[:], in0=m4[:, 0:2], in1=m4[:, 2:4], op=ALU.max)
-            m1 = trees.tile([P, J * D], BF16)
-            nc.vector.tensor_tensor(out=m1[:], in0=m2[:, 0], in1=m2[:, 1], op=ALU.max)
-
-            flat = r_t[:].rearrange("p k j d -> p k (j d)")
-            sum_a = trees.tile([P, J * D], F32)
-            sum_b = trees.tile([P, J * D], F32)
-            nc.vector.tensor_tensor(out=sum_a[:], in0=flat[:, 0], in1=flat[:, 1], op=ALU.add)
-            nc.vector.tensor_tensor(out=sum_b[:], in0=flat[:, 4], in1=flat[:, 5], op=ALU.add)
-            for k in (2, 3):
-                nc.vector.tensor_tensor(out=sum_a[:], in0=sum_a[:], in1=flat[:, k], op=ALU.add)
-                nc.vector.tensor_tensor(out=sum_b[:], in0=sum_b[:], in1=flat[:, k + 4], op=ALU.add)
-            nc.vector.tensor_tensor(out=sum_a[:], in0=sum_a[:], in1=sum_b[:], op=ALU.add)
-            nc.vector.scalar_tensor_tensor(
-                out=sum_a[:], in0=sum_a[:], scalar=MEAN_W / REFS / MAX_W, in1=m1[:], op0=ALU.mult, op1=ALU.add
-            )
+            nc.vector.tensor_tensor(out=m4[:, 0:2], in0=m4[:, 0:2], in1=m4[:, 2:4], op=ALU.max)
+            nc.vector.tensor_tensor(out=m4[:, 0], in0=m4[:, 0], in1=m4[:, 1], op=ALU.max)
 
             for j in range(J):
                 t = b * J + j
-                pooled = work.tile([P, D], BF16)
-                nc.scalar.activation(
-                    out=pooled[:], in_=sum_a[:, j * D : (j + 1) * D], func=ACT.Copy, scale=s_max[:, t : t + 1]
+                wide = terms.tile([P, TERMS, HALF_PASSES, PACK, P], F32)
+                for k in range(REFS):
+                    src = r_t[:, k, j, :].rearrange("p (g q i) -> p g i q", g=HALF_PASSES, i=PACK)
+                    if k < SCALAR_TERMS:
+                        nc.scalar.activation(out=wide[:, k], in_=src, func=ACT.Copy, scale=s_mean[:, t : t + 1])
+                    else:
+                        nc.vector.tensor_scalar_mul(out=wide[:, k], in0=src, scalar1=s_mean[:, t : t + 1])
+                nc.vector.tensor_scalar_mul(
+                    out=wide[:, REFS],
+                    in0=m4[:, 0, j * D : (j + 1) * D].rearrange("p (g q i) -> p g i q", g=HALF_PASSES, i=PACK),
+                    scalar1=s_max[:, t : t + 1],
                 )
 
                 grouped = work.tile([P, PASSES, P, PACK], BF16, align_bytes=64)
                 o_words = o_t[:, j, :].bitcast(F32)
-                oT_ps = psum.tile([P, HALF_PASSES, 2, P], F32, tag="xt")
+                oT_ps = psum.tile([P, HALF_PASSES, 2, P], F32, tag="oT")
                 for g in range(HALF_PASSES):
                     for u in range(2):
                         nc.tensor.transpose(
@@ -172,13 +170,19 @@ def tile_rarevariantawarefusion_pa_kernel(
                     .rearrange("p (g r u) -> p g r u", g=HALF_PASSES, u=2)
                 )
                 nc.scalar.copy(out=o_grouped, in_=oT_ps[:].rearrange("p g u r -> p g r u"))
-                pT_ps = psum.tile([P, HALF_PASSES, PACK, P], BF16, tag="xt")
                 for g in range(HALF_PASSES):
+                    pT_ps = psum.tile([P, PACK, P], F32, tag="pT", bufs=4)
                     for i in range(PACK):
-                        nc.tensor.transpose(
-                            pT_ps[:, g, i, :], pooled[:, K_PASS * g + i : K_PASS * (g + 1) : PACK], ident_bf[:]
-                        )
-                nc.scalar.copy(out=grouped[:, HALF_PASSES:PASSES], in_=pT_ps[:].rearrange("p g i r -> p g r i"))
+                        for term in range(TERMS):
+                            nc.tensor.matmul(
+                                pT_ps[:, i, :],
+                                lhsT=wide[:, term, g, i, :],
+                                rhs=ident_f32[:],
+                                is_transpose=True,
+                                start=(term == 0),
+                                stop=(term == TERMS - 1),
+                            )
+                    nc.scalar.copy(out=grouped[:, HALF_PASSES + g], in_=pT_ps[:].rearrange("p i r -> p r i"))
 
                 x_codes = work.tile([P, PASSES * P], U32, align_bytes=64)
                 x_planes = work.tile([P, PASSES * P], U8, align_bytes=64)
@@ -189,7 +193,7 @@ def tile_rarevariantawarefusion_pa_kernel(
                 )
 
                 y = work.tile([P, D], F32, tag="y")
-                stats = work.tile([P, N_HALVES, 6], F32)
+                y_sum = work.tile([P, N_HALVES], F32)
                 for n in range(N_HALVES):
                     cols = slice(n * N_TILE, (n + 1) * N_TILE)
                     acc = psum.tile([P, N_TILE], F32, tag="acc")
@@ -203,24 +207,39 @@ def tile_rarevariantawarefusion_pa_kernel(
                             start=(g == 0),
                             stop=(g == PASSES - 1),
                         )
-                    nc.vector.tensor_tensor(out=y[:, cols], in0=acc[:], in1=biasf_bc[:, cols], op=ALU.add)
-                    nc.vector.bn_stats(out=stats[:, n, :], in_=y[:, cols])
-                mean_var = work.tile([P, 2], F32)
-                nc.vector.bn_aggr(out=mean_var[:], in_=stats[:].rearrange("p n s -> p (n s)"))
+                    nc.vector.scalar_tensor_tensor(
+                        out=y[:, cols],
+                        in0=acc[:],
+                        scalar=1.0,
+                        in1=biasf_bc[:, cols],
+                        op0=ALU.mult,
+                        op1=ALU.add,
+                        accum_out=y_sum[:, n : n + 1],
+                    )
+                neg_mean = work.tile([P, 1], F32)
+                nc.vector.tensor_scalar(
+                    out=neg_mean[:], in0=y_sum[:, 0:1], scalar1=y_sum[:, 1:2], scalar2=-1.0 / D, op0=ALU.add, op1=ALU.mult
+                )
+                squares = work.tile([P, D], BF16, tag="gates")
+                sq_sum = work.tile([P, 1], F32)
+                nc.scalar.activation(
+                    out=squares[:], in_=y[:], func=ACT.Square, bias=neg_mean[:], accum_out=sq_sum[:]
+                )
                 var_eps = work.tile([P, 1], F32)
-                nc.vector.tensor_scalar_add(out=var_eps[:], in0=mean_var[:, 1:2], scalar1=LN_EPS)
+                nc.gpsimd.tensor_scalar(
+                    out=var_eps[:], in0=sq_sum[:], scalar1=1.0 / D, scalar2=LN_EPS, op0=ALU.mult, op1=ALU.add
+                )
                 rstd = work.tile([P, 1], F32)
                 nc.gpsimd.tensor_tensor(out=rstd[:], in0=var_eps[:], in1=neg_half[:], op=ALU.pow)
                 nc.vector.scalar_tensor_tensor(
-                    out=y[:], in0=y[:], scalar=mean_var[:, 0:1], in1=lng_bc[:], op0=ALU.subtract, op1=ALU.mult
+                    out=y[:], in0=y[:], scalar=neg_mean[:], in1=lng_bc[:], op0=ALU.add, op1=ALU.mult
                 )
                 nc.vector.scalar_tensor_tensor(
                     out=y[:], in0=y[:], scalar=rstd[:], in1=lnb_bc[:], op0=ALU.mult, op1=ALU.add
                 )
-                fused = work.tile([P, D], F32)
-                nc.scalar.activation(out=fused[:], in_=y[:], func=ACT.Gelu)
+                nc.scalar.activation(out=y[:], in_=y[:], func=ACT.Gelu)
                 res = work.tile([P, D], F32)
                 nc.vector.scalar_tensor_tensor(
-                    out=res[:], in0=fused[:], scalar=af_scale[:, t : t + 1], in1=o_t[:, j, :], op0=ALU.mult, op1=ALU.add
+                    out=res[:], in0=y[:], scalar=af_scale[:, t : t + 1], in1=o_t[:, j, :], op0=ALU.mult, op1=ALU.add
                 )
                 nc.sync.dma_start(out=out[b].rearrange("(p j) d -> p j d", j=J)[:, j, :], in_=res[:])

@@ -17,6 +17,7 @@ P = 128
 B, REFS, L, D, H = 4, 8, 256, 1024, 128
 J = L // P
 TILES = B * J
+BLOCKS = D // P
 PACK = 4
 K_PASS = P * PACK
 PASSES = 2 * D // K_PASS
@@ -26,7 +27,10 @@ N_HALVES = D // N_TILE
 LN_EPS = 1e-5
 MEAN_W, MAX_W = 0.7, 0.3
 TERMS = REFS + 1
-SCALAR_TERMS = 5
+SCALAR_TERMS = 6
+CHUNKS = 4
+RAG_BUFS = 4
+GATES_AHEAD = 4
 
 FLOPS = 2 * B * L * (2 * D) * D + 2 * B * L * H * D
 
@@ -38,17 +42,31 @@ def tile_rarevariantawarefusion_pa_kernel(
     with ExitStack() as ctx:
         const = ctx.enter_context(tc.tile_pool(name="const", bufs=1))
         origs = ctx.enter_context(tc.tile_pool(name="origs", bufs=B))
-        rags = ctx.enter_context(tc.tile_pool(name="rags", bufs=2))
-        trees = ctx.enter_context(tc.tile_pool(name="trees", bufs=1))
+        rags = ctx.enter_context(tc.tile_pool(name="rags", bufs=RAG_BUFS))
         terms = ctx.enter_context(tc.tile_pool(name="terms", bufs=2))
         work = ctx.enter_context(tc.tile_pool(name="work", bufs=2))
         psum = ctx.enter_context(tc.psum_pool(name="psum", bufs=2))
+        ctx.enter_context(tc.manual_schedule())
 
-        w_planes = const.tile([P, PASSES, D], U8, align_bytes=64)
-        nc.vector.memset(w_planes[:].bitcast(I32), 0)
-        scale_rows = wf_scales.bitcast(I32).rearrange("g (q r) n -> r q g n", r=4)
-        for r in range(4):
-            nc.sync.dma_start(out=w_planes[:].bitcast(I32)[r:P:32], in_=scale_rows[r])
+        orig_sb, refs, maxima, wide, orig_t, pooled_t, grouped = {}, {}, {}, {}, {}, {}, {}
+        x_codes, x_planes, acc, y, y_sum, neg_mean, rstd = {}, {}, {}, {}, {}, {}, {}
+
+        def live(t):
+            return 0 <= t < TILES
+
+        def load_orig(b):
+            o_t = origs.tile([P, J, D], BF16, name="o_t")
+            nc.sync.dma_start(
+                out=o_t[:].rearrange("p j d -> p (j d)"), in_=orig_feat[b].rearrange("(p j) d -> p (j d)", j=J)
+            )
+            orig_sb[b] = o_t
+
+        def load_refs(t):
+            r_t = rags.tile([P, REFS, D], BF16, name="r_t")
+            rows = rag_feat[t // J].rearrange("k (p j) d -> j p k d", j=J)[t % J]
+            for k in range(0, REFS, REFS // 2):
+                nc.sync.dma_start(out=r_t[:, k : k + REFS // 2], in_=rows[:, k : k + REFS // 2])
+            refs[t] = r_t
 
         haf = const.tile([P, B, J, H], BF16)
         nc.sync.dma_start(
@@ -56,190 +74,277 @@ def tile_rarevariantawarefusion_pa_kernel(
         )
         w2_sb = const.tile([P, D], BF16)
         nc.sync.dma_start(out=w2_sb[:], in_=w2)
+        vec_rows = const.tile([P, P], BF16)
+        nc.vector.memset(vec_rows[:], 0.0)
+        for v, vec in enumerate((b2, bias_f, ln_g, ln_b)):
+            nc.sync.dma_start(out=vec_rows[v * BLOCKS : (v + 1) * BLOCKS, :], in_=vec.rearrange("(c m) -> c m", m=P))
         af_sb = const.tile([P, B, J], BF16)
         nc.sync.dma_start(out=af_sb[:], in_=af.rearrange("b (p j) -> p b j", j=J))
+        load_refs(0)
+        load_orig(0)
+        load_refs(1)
+        w_planes = const.tile([P, PASSES, D], U8, align_bytes=64)
+        nc.vector.memset(w_planes[:].bitcast(I32), 0)
+        scale_rows = wf_scales.bitcast(I32).rearrange("g (q r) n -> r q g n", r=4)
+        for r in range(4):
+            nc.sync.dma_start(out=w_planes[:].bitcast(I32)[r:P:32], in_=scale_rows[r])
+        w_words = const.tile([P, PASSES, 2 * D], U8, align_bytes=64)
+        nc.sync.dma_start(out=w_words[:].bitcast(I32), in_=wf_words.rearrange("g p n -> p g n").bitcast(I32))
+        load_refs(2)
+        load_orig(1)
+        load_refs(3)
 
-        b2_bc = const.tile([P, D], BF16)
-        nc.scalar.dma_start(out=b2_bc[:], in_=b2.partition_broadcast(P))
-        biasf_bc = const.tile([P, D], BF16)
-        nc.scalar.dma_start(out=biasf_bc[:], in_=bias_f.partition_broadcast(P))
-        lng_bc = const.tile([P, D], BF16)
-        nc.scalar.dma_start(out=lng_bc[:], in_=ln_g.partition_broadcast(P))
-        lnb_bc = const.tile([P, D], BF16)
-        nc.scalar.dma_start(out=lnb_bc[:], in_=ln_b.partition_broadcast(P))
-
-        ident_f32 = const.tile([P, P], F32)
-        make_identity(nc, ident_f32[:])
         ident_bf = const.tile([P, P], BF16)
         make_identity(nc, ident_bf[:])
+        ident_f32 = const.tile([P, P], F32)
+        make_identity(nc, ident_f32[:])
+        half = const.tile([P, TILES], F32)
+        nc.vector.memset(half[:], 0.5)
+        neg_half = const.tile([P, 1], F32)
+        nc.vector.memset(neg_half[:], -0.5)
 
-        orig_sb = []
-        rag_sb = []
-        w_words = const.tile([P, PASSES, 2 * D], U8, align_bytes=64)
+        cols_ps = psum.tile([P, P], BF16, tag="oT")
+        nc.tensor.transpose(cols_ps[:], vec_rows[:], ident_bf[:])
+        vec_cols = const.tile([P, 4 * BLOCKS], BF16)
+        nc.vector.tensor_copy(out=vec_cols[:], in_=cols_ps[:, 0 : 4 * BLOCKS])
 
-        def load_batch(b):
-            o_t = origs.tile([P, J, D], BF16, name="o_t")
-            nc.sync.dma_start(
-                out=o_t[:].rearrange("p j d -> p (j d)"), in_=orig_feat[b].rearrange("(p j) d -> p (j d)", j=J)
-            )
-            orig_sb.append(o_t)
-            r_t = rags.tile([P, REFS, J, D], BF16, name="r_t")
-            rows = rag_feat[b].rearrange("k (p j) d -> p k (j d)", j=J)
-            for k in range(0, REFS, 2):
-                nc.sync.dma_start(out=r_t[:, k : k + 2].rearrange("p k j d -> p k (j d)"), in_=rows[:, k : k + 2])
-            rag_sb.append(r_t)
-
-        load_batch(0)
-        nc.sync.dma_start(out=w_words[:].bitcast(I32), in_=wf_words.rearrange("g p n -> p g n").bitcast(I32))
+        def spread(v):
+            spread_ps = psum.tile([P, BLOCKS, P], BF16, tag="oT")
+            for c in range(BLOCKS):
+                col = v * BLOCKS + c
+                nc.tensor.transpose(spread_ps[:, c, :], vec_cols[:, col : col + 1].to_broadcast([P, P]), ident_bf[:])
+            everywhere = const.tile([P, D], BF16, name="everywhere%d" % v)
+            nc.vector.tensor_copy(out=everywhere[:], in_=spread_ps[:].rearrange("p c m -> p (c m)"))
+            return everywhere
 
         hT_ps = psum.tile([P, TILES, P], BF16, tag="oT")
         for t in range(TILES):
             nc.tensor.transpose(hT_ps[:, t, :], haf[:, t // J, t % J, :], ident_bf[:])
         hT = const.tile([P, TILES, P], BF16)
         nc.vector.tensor_copy(out=hT[:], in_=hT_ps[:])
+        b2_bc = spread(0)
         s_all = const.tile([P, TILES], F32)
-        for t in range(TILES):
+
+        def gate(t):
             logits = work.tile([P, D], F32, tag="y")
             for n in range(N_HALVES):
                 cols = slice(n * N_TILE, (n + 1) * N_TILE)
                 z_ps = psum.tile([P, N_TILE], F32, tag="acc")
                 nc.tensor.matmul(z_ps[:], lhsT=hT[:, t, :], rhs=w2_sb[:, cols], start=True, stop=True)
                 nc.vector.tensor_tensor(out=logits[:, cols], in0=z_ps[:], in1=b2_bc[:, cols], op=ALU.add)
-            gates = work.tile([P, D], BF16, tag="gates")
+            gates = work.tile([P, D], BF16, tag="unread")
             nc.scalar.activation(out=gates[:], in_=logits[:], func=ACT.Sigmoid, accum_out=s_all[:, t : t + 1])
-        s_max = const.tile([P, TILES], F32)
-        nc.vector.tensor_scalar_mul(out=s_max[:], in0=s_all[:], scalar1=MAX_W)
-        s_mean = const.tile([P, TILES], F32)
-        nc.vector.tensor_scalar_mul(out=s_mean[:], in0=s_all[:], scalar1=MEAN_W / REFS)
 
-        half = const.tile([P, TILES], F32)
-        nc.vector.memset(half[:], 0.5)
-        neg_half = const.tile([P, 1], F32)
-        nc.vector.memset(neg_half[:], -0.5)
+        for t in range(GATES_AHEAD):
+            gate(t)
+        biasf_bc = spread(1)
+        lng_bc = spread(2)
+        lnb_bc = spread(3)
+
         af_flat = af_sb[:].rearrange("p b j -> p (b j)")
         one_minus = const.tile([P, TILES], F32)
         nc.vector.tensor_scalar(out=one_minus[:], in0=af_flat, scalar1=-1.0, scalar2=1.0, op0=ALU.mult, op1=ALU.add)
-        spread = const.tile([P, TILES], F32)
-        nc.vector.tensor_tensor(out=spread[:], in0=one_minus[:], in1=af_flat, op=ALU.mult)
+        spread_af = const.tile([P, TILES], F32)
+        nc.vector.tensor_tensor(out=spread_af[:], in0=one_minus[:], in1=af_flat, op=ALU.mult)
         af_scale = const.tile([P, TILES], F32)
-        nc.gpsimd.tensor_tensor(out=af_scale[:], in0=spread[:], in1=half[:], op=ALU.pow)
+        nc.gpsimd.tensor_tensor(out=af_scale[:], in0=spread_af[:], in1=half[:], op=ALU.pow)
 
-        for b in range(B):
-            if b + 1 < B:
-                load_batch(b + 1)
-            o_t = orig_sb[b]
-            r_t = rag_sb[b]
-
-            m4 = trees.tile([P, 4, J * D], BF16)
-            nc.vector.tensor_tensor(
-                out=m4[:],
-                in0=r_t[:, 0:4].rearrange("p k j d -> p k (j d)"),
-                in1=r_t[:, 4:8].rearrange("p k j d -> p k (j d)"),
-                op=ALU.max,
-            )
+        def max_tree(t):
+            r_t = refs[t]
+            m4 = work.tile([P, 4, D], BF16)
+            nc.vector.tensor_tensor(out=m4[:], in0=r_t[:, 0:4], in1=r_t[:, 4:8], op=ALU.max)
             nc.vector.tensor_tensor(out=m4[:, 0:2], in0=m4[:, 0:2], in1=m4[:, 2:4], op=ALU.max)
             nc.vector.tensor_tensor(out=m4[:, 0], in0=m4[:, 0], in1=m4[:, 1], op=ALU.max)
+            maxima[t] = m4
+            wide[t] = terms.tile([P, TERMS, HALF_PASSES, PACK, P], F32, name="wide")
 
-            for j in range(J):
-                t = b * J + j
-                wide = terms.tile([P, TERMS, HALF_PASSES, PACK, P], F32)
-                for k in range(REFS):
-                    src = r_t[:, k, j, :].rearrange("p (g q i) -> p g i q", g=HALF_PASSES, i=PACK)
-                    if k < SCALAR_TERMS:
-                        nc.scalar.activation(out=wide[:, k], in_=src, func=ACT.Copy, scale=s_mean[:, t : t + 1])
-                    else:
-                        nc.vector.tensor_scalar_mul(out=wide[:, k], in0=src, scalar1=s_mean[:, t : t + 1])
-                nc.vector.tensor_scalar_mul(
-                    out=wide[:, REFS],
-                    in0=m4[:, 0, j * D : (j + 1) * D].rearrange("p (g q i) -> p g i q", g=HALF_PASSES, i=PACK),
-                    scalar1=s_max[:, t : t + 1],
-                )
+        def by_word(row):
+            return row.rearrange("p (g q i) -> p g i q", g=HALF_PASSES, i=PACK)
 
-                grouped = work.tile([P, PASSES, P, PACK], BF16, align_bytes=64)
-                o_words = o_t[:, j, :].bitcast(F32)
-                oT_ps = psum.tile([P, HALF_PASSES, 2, P], F32, tag="oT")
-                for g in range(HALF_PASSES):
-                    for u in range(2):
-                        nc.tensor.transpose(
-                            oT_ps[:, g, u, :], o_words[:, 256 * g + u : 256 * (g + 1) : 2], ident_f32[:]
-                        )
-                o_grouped = (
-                    grouped[:, 0:HALF_PASSES]
-                    .rearrange("p g r i -> p (g r i)")
-                    .bitcast(F32)
-                    .rearrange("p (g r u) -> p g r u", g=HALF_PASSES, u=2)
-                )
-                nc.scalar.copy(out=o_grouped, in_=oT_ps[:].rearrange("p g u r -> p g r u"))
-                for g in range(HALF_PASSES):
-                    pT_ps = psum.tile([P, PACK, P], F32, tag="pT", bufs=4)
-                    for i in range(PACK):
-                        for term in range(TERMS):
-                            nc.tensor.matmul(
-                                pT_ps[:, i, :],
-                                lhsT=wide[:, term, g, i, :],
-                                rhs=ident_f32[:],
-                                is_transpose=True,
-                                start=(term == 0),
-                                stop=(term == TERMS - 1),
-                            )
-                    nc.scalar.copy(out=grouped[:, HALF_PASSES + g], in_=pT_ps[:].rearrange("p i r -> p r i"))
-
-                x_codes = work.tile([P, PASSES * P], U32, align_bytes=64)
-                x_planes = work.tile([P, PASSES * P], U8, align_bytes=64)
-                nc.vector.quantize_mx(
-                    out=x_codes[:].bitcast(FP8X4),
-                    scales=x_planes[:],
-                    in_=grouped[:].rearrange("p g r i -> p (g r i)"),
-                )
-
-                y = work.tile([P, D], F32, tag="y")
-                y_sum = work.tile([P, N_HALVES], F32)
-                for n in range(N_HALVES):
-                    cols = slice(n * N_TILE, (n + 1) * N_TILE)
-                    acc = psum.tile([P, N_TILE], F32, tag="acc")
-                    for g in range(PASSES):
-                        nc.tensor.matmul_mx(
-                            out=acc[:],
-                            lhsT=x_codes[:, g * P : (g + 1) * P].bitcast(FP8X4),
-                            lhsT_scale=x_planes[:, g * P : (g + 1) * P],
-                            rhs=w_words[:, g, 2 * n * N_TILE : 2 * (n + 1) * N_TILE].bitcast(FP4X4),
-                            rhs_scale=w_planes[:, g, cols],
-                            start=(g == 0),
-                            stop=(g == PASSES - 1),
-                        )
-                    nc.vector.scalar_tensor_tensor(
-                        out=y[:, cols],
-                        in0=acc[:],
-                        scalar=1.0,
-                        in1=biasf_bc[:, cols],
+        def widen(t, first, last):
+            s_t = s_all[:, t : t + 1]
+            for k in range(first, last):
+                if k < SCALAR_TERMS:
+                    nc.scalar.activation(out=wide[t][:, k], in_=by_word(refs[t][:, k, :]), func=ACT.Copy, scale=s_t)
+                elif k < REFS:
+                    nc.vector.tensor_scalar_mul(out=wide[t][:, k], in0=by_word(refs[t][:, k, :]), scalar1=s_t)
+                else:
+                    nc.vector.tensor_scalar(
+                        out=wide[t][:, k],
+                        in0=by_word(maxima[t][:, 0, :]),
+                        scalar1=s_t,
+                        scalar2=MAX_W * REFS / MEAN_W,
                         op0=ALU.mult,
-                        op1=ALU.add,
-                        accum_out=y_sum[:, n : n + 1],
+                        op1=ALU.mult,
                     )
-                neg_mean = work.tile([P, 1], F32)
-                nc.vector.tensor_scalar(
-                    out=neg_mean[:], in0=y_sum[:, 0:1], scalar1=y_sum[:, 1:2], scalar2=-1.0 / D, op0=ALU.add, op1=ALU.mult
+
+        def turn_orig(t):
+            o_words = orig_sb[t // J][:, t % J, :].bitcast(F32)
+            orig_t[t] = psum.tile([P, HALF_PASSES, 2, P], F32, tag="oT", name="orig_t")
+            for g in range(HALF_PASSES):
+                for u in range(2):
+                    nc.tensor.transpose(orig_t[t][:, g, u, :], o_words[:, 256 * g + u : 256 * (g + 1) : 2], ident_f32[:])
+
+        def turn_pooled(t, chunk):
+            g = chunk * HALF_PASSES // CHUNKS
+            per_chunk = HALF_PASSES * PACK // CHUNKS
+            if chunk * HALF_PASSES % CHUNKS == 0:
+                pooled_t[t, g] = psum.tile([P, PACK, P], F32, tag="pT", bufs=4, name="pooled_t")
+            for i in range(chunk * per_chunk % PACK, chunk * per_chunk % PACK + per_chunk):
+                for term in range(TERMS):
+                    nc.tensor.matmul(
+                        pooled_t[t, g][:, i, :],
+                        lhsT=wide[t][:, term, g, i, :],
+                        rhs=ident_f32[:],
+                        is_transpose=True,
+                        start=(term == 0),
+                        stop=(term == TERMS - 1),
+                    )
+
+        def copy_out_orig(t):
+            grouped[t] = work.tile([P, PASSES, P, PACK], BF16, align_bytes=64, name="grouped")
+            o_grouped = (
+                grouped[t][:, 0:HALF_PASSES]
+                .rearrange("p g r i -> p (g r i)")
+                .bitcast(F32)
+                .rearrange("p (g r u) -> p g r u", g=HALF_PASSES, u=2)
+            )
+            nc.scalar.copy(out=o_grouped, in_=orig_t[t][:].rearrange("p g u r -> p g r u"))
+
+        def copy_out_pooled(t, g):
+            nc.scalar.activation(
+                out=grouped[t][:, HALF_PASSES + g],
+                in_=pooled_t[t, g][:].rearrange("p i r -> p r i"),
+                func=ACT.Copy,
+                scale=MEAN_W / REFS,
+            )
+
+        def quantise(t):
+            x_codes[t] = work.tile([P, PASSES * P], U32, align_bytes=64, name="x_codes")
+            x_planes[t] = work.tile([P, PASSES * P], U8, align_bytes=64, name="x_planes")
+            nc.vector.quantize_mx(
+                out=x_codes[t][:].bitcast(FP8X4),
+                scales=x_planes[t][:],
+                in_=grouped[t][:].rearrange("p g r i -> p (g r i)"),
+            )
+
+        def multiply(t, chunk):
+            n = chunk * N_HALVES // CHUNKS
+            per_chunk = N_HALVES * PASSES // CHUNKS
+            if chunk * N_HALVES % CHUNKS == 0:
+                acc[t, n] = psum.tile([P, N_TILE], F32, tag="acc", name="acc")
+            for g in range(chunk * per_chunk % PASSES, chunk * per_chunk % PASSES + per_chunk):
+                nc.tensor.matmul_mx(
+                    out=acc[t, n][:],
+                    lhsT=x_codes[t][:, g * P : (g + 1) * P].bitcast(FP8X4),
+                    lhsT_scale=x_planes[t][:, g * P : (g + 1) * P],
+                    rhs=w_words[:, g, 2 * n * N_TILE : 2 * (n + 1) * N_TILE].bitcast(FP4X4),
+                    rhs_scale=w_planes[:, g, n * N_TILE : (n + 1) * N_TILE],
+                    start=(g == 0),
+                    stop=(g == PASSES - 1),
                 )
-                squares = work.tile([P, D], BF16, tag="gates")
-                sq_sum = work.tile([P, 1], F32)
-                nc.scalar.activation(
-                    out=squares[:], in_=y[:], func=ACT.Square, bias=neg_mean[:], accum_out=sq_sum[:]
-                )
-                var_eps = work.tile([P, 1], F32)
-                nc.gpsimd.tensor_scalar(
-                    out=var_eps[:], in0=sq_sum[:], scalar1=1.0 / D, scalar2=LN_EPS, op0=ALU.mult, op1=ALU.add
-                )
-                rstd = work.tile([P, 1], F32)
-                nc.gpsimd.tensor_tensor(out=rstd[:], in0=var_eps[:], in1=neg_half[:], op=ALU.pow)
-                nc.vector.scalar_tensor_tensor(
-                    out=y[:], in0=y[:], scalar=neg_mean[:], in1=lng_bc[:], op0=ALU.add, op1=ALU.mult
-                )
-                nc.vector.scalar_tensor_tensor(
-                    out=y[:], in0=y[:], scalar=rstd[:], in1=lnb_bc[:], op0=ALU.mult, op1=ALU.add
-                )
-                nc.scalar.activation(out=y[:], in_=y[:], func=ACT.Gelu)
-                res = work.tile([P, D], F32)
-                nc.vector.scalar_tensor_tensor(
-                    out=res[:], in0=y[:], scalar=af_scale[:, t : t + 1], in1=o_t[:, j, :], op0=ALU.mult, op1=ALU.add
-                )
-                nc.sync.dma_start(out=out[b].rearrange("(p j) d -> p j d", j=J)[:, j, :], in_=res[:])
+
+        def add_bias(t, n):
+            if n == 0:
+                y[t] = work.tile([P, D], F32, tag="y", name="y")
+                y_sum[t] = work.tile([P, N_HALVES], F32, name="y_sum")
+            cols = slice(n * N_TILE, (n + 1) * N_TILE)
+            nc.vector.scalar_tensor_tensor(
+                out=y[t][:, cols],
+                in0=acc[t, n][:],
+                scalar=1.0,
+                in1=biasf_bc[:, cols],
+                op0=ALU.mult,
+                op1=ALU.add,
+                accum_out=y_sum[t][:, n : n + 1],
+            )
+
+        def mean(t):
+            neg_mean[t] = work.tile([P, 1], F32, name="neg_mean")
+            nc.vector.tensor_scalar(
+                out=neg_mean[t][:],
+                in0=y_sum[t][:, 0:1],
+                scalar1=y_sum[t][:, 1:2],
+                scalar2=-1.0 / D,
+                op0=ALU.add,
+                op1=ALU.mult,
+            )
+
+        def variance(t):
+            squares = work.tile([P, D], BF16, tag="unread")
+            sq_sum = work.tile([P, 1], F32)
+            nc.scalar.activation(out=squares[:], in_=y[t][:], func=ACT.Square, bias=neg_mean[t][:], accum_out=sq_sum[:])
+            var_eps = work.tile([P, 1], F32)
+            nc.gpsimd.tensor_scalar(
+                out=var_eps[:], in0=sq_sum[:], scalar1=1.0 / D, scalar2=LN_EPS, op0=ALU.mult, op1=ALU.add
+            )
+            rstd[t] = work.tile([P, 1], F32, name="rstd")
+            nc.gpsimd.tensor_tensor(out=rstd[t][:], in0=var_eps[:], in1=neg_half[:], op=ALU.pow)
+
+        def affine(t):
+            nc.vector.scalar_tensor_tensor(
+                out=y[t][:], in0=y[t][:], scalar=neg_mean[t][:], in1=lng_bc[:], op0=ALU.add, op1=ALU.mult
+            )
+            nc.vector.scalar_tensor_tensor(
+                out=y[t][:], in0=y[t][:], scalar=rstd[t][:], in1=lnb_bc[:], op0=ALU.mult, op1=ALU.add
+            )
+
+        def gelu(t):
+            nc.scalar.activation(out=y[t][:], in_=y[t][:], func=ACT.Gelu)
+
+        def residual(t):
+            res = work.tile([P, D], F32)
+            nc.vector.scalar_tensor_tensor(
+                out=res[:],
+                in0=y[t][:],
+                scalar=af_scale[:, t : t + 1],
+                in1=orig_sb[t // J][:, t % J, :],
+                op0=ALU.mult,
+                op1=ALU.add,
+            )
+            nc.sync.dma_start(out=out[t // J].rearrange("(p j) d -> p j d", j=J)[:, t % J, :], in_=res[:])
+
+        def tensor_chunk(turning, multiplying, chunk):
+            if live(turning):
+                if chunk == 0:
+                    turn_orig(turning)
+                turn_pooled(turning, chunk)
+            if live(multiplying):
+                multiply(multiplying, chunk)
+
+        for step in range(TILES + 3):
+            widening, turning, multiplying, norming = step, step - 1, step - 2, step - 3
+            if live(multiplying):
+                copy_out_pooled(multiplying, 1)
+                quantise(multiplying)
+            if live(norming):
+                variance(norming)
+            if live(widening):
+                max_tree(widening)
+                widen(widening, 0, 4)
+            if live(norming):
+                affine(norming)
+            tensor_chunk(turning, multiplying, 0)
+            tensor_chunk(turning, multiplying, 1)
+            if live(multiplying):
+                add_bias(multiplying, 0)
+            if live(norming):
+                gelu(norming)
+            if live(widening):
+                widen(widening, 4, TERMS)
+            if live(norming):
+                residual(norming)
+            if live(widening + RAG_BUFS):
+                load_refs(widening + RAG_BUFS)
+                if (widening + RAG_BUFS) % J == 0:
+                    load_orig((widening + RAG_BUFS) // J)
+            tensor_chunk(turning, multiplying, 2)
+            tensor_chunk(turning, multiplying, 3)
+            if live(turning):
+                copy_out_orig(turning)
+                copy_out_pooled(turning, 0)
+            if live(multiplying):
+                add_bias(multiplying, 1)
+                mean(multiplying)
+            for t in range(GATES_AHEAD + 2 * step, min(GATES_AHEAD + 2 * step + 2, TILES)):
+                gate(t)

@@ -26,9 +26,8 @@ N_TILE = 512
 N_HALVES = D // N_TILE
 LN_EPS = 1e-5
 MEAN_W, MAX_W = 0.7, 0.3
-TERMS = REFS + 1
 SCALAR_TERMS = 6
-CHUNKS = 4
+TERMS = SCALAR_TERMS + 1
 RAG_BUFS = 4
 GATES_AHEAD = 4
 
@@ -48,7 +47,7 @@ def tile_rarevariantawarefusion_pa_kernel(
         psum = ctx.enter_context(tc.psum_pool(name="psum", bufs=2))
         ctx.enter_context(tc.manual_schedule())
 
-        orig_sb, refs, maxima, wide, orig_t, pooled_t, grouped = {}, {}, {}, {}, {}, {}, {}
+        orig_sb, refs, rest, maxima, wide, orig_t, pooled_t, grouped = {}, {}, {}, {}, {}, {}, {}, {}
         x_codes, x_planes, acc, y, y_sum, neg_mean, rstd = {}, {}, {}, {}, {}, {}, {}
 
         def live(t):
@@ -149,6 +148,12 @@ def tile_rarevariantawarefusion_pa_kernel(
         af_scale = const.tile([P, TILES], F32)
         nc.gpsimd.tensor_tensor(out=af_scale[:], in0=spread_af[:], in1=half[:], op=ALU.pow)
 
+        def sum_rest(t):
+            rest[t] = work.tile([P, D], F32, name="rest")
+            nc.vector.tensor_tensor(
+                out=rest[t][:], in0=refs[t][:, SCALAR_TERMS, :], in1=refs[t][:, SCALAR_TERMS + 1, :], op=ALU.add
+            )
+
         def max_tree(t):
             r_t = refs[t]
             m4 = work.tile([P, 4, D], BF16)
@@ -162,21 +167,21 @@ def tile_rarevariantawarefusion_pa_kernel(
             return row.rearrange("p (g q i) -> p g i q", g=HALF_PASSES, i=PACK)
 
         def widen(t, first, last):
-            s_t = s_all[:, t : t + 1]
             for k in range(first, last):
-                if k < SCALAR_TERMS:
-                    nc.scalar.activation(out=wide[t][:, k], in_=by_word(refs[t][:, k, :]), func=ACT.Copy, scale=s_t)
-                elif k < REFS:
-                    nc.vector.tensor_scalar_mul(out=wide[t][:, k], in0=by_word(refs[t][:, k, :]), scalar1=s_t)
-                else:
-                    nc.vector.tensor_scalar(
-                        out=wide[t][:, k],
-                        in0=by_word(maxima[t][:, 0, :]),
-                        scalar1=s_t,
-                        scalar2=MAX_W * REFS / MEAN_W,
-                        op0=ALU.mult,
-                        op1=ALU.mult,
-                    )
+                nc.scalar.activation(
+                    out=wide[t][:, k], in_=by_word(refs[t][:, k, :]), func=ACT.Copy, scale=s_all[:, t : t + 1]
+                )
+
+        def widen_rest(t):
+            nc.vector.scalar_tensor_tensor(
+                out=rest[t][:],
+                in0=maxima[t][:, 0, :],
+                scalar=MAX_W * REFS / MEAN_W,
+                in1=rest[t][:],
+                op0=ALU.mult,
+                op1=ALU.add,
+            )
+            nc.vector.tensor_scalar_mul(out=wide[t][:, SCALAR_TERMS], in0=by_word(rest[t][:]), scalar1=s_all[:, t : t + 1])
 
         def turn_orig(t):
             o_words = orig_sb[t // J][:, t % J, :].bitcast(F32)
@@ -185,12 +190,9 @@ def tile_rarevariantawarefusion_pa_kernel(
                 for u in range(2):
                     nc.tensor.transpose(orig_t[t][:, g, u, :], o_words[:, 256 * g + u : 256 * (g + 1) : 2], ident_f32[:])
 
-        def turn_pooled(t, chunk):
-            g = chunk * HALF_PASSES // CHUNKS
-            per_chunk = HALF_PASSES * PACK // CHUNKS
-            if chunk * HALF_PASSES % CHUNKS == 0:
-                pooled_t[t, g] = psum.tile([P, PACK, P], F32, tag="pT", bufs=4, name="pooled_t")
-            for i in range(chunk * per_chunk % PACK, chunk * per_chunk % PACK + per_chunk):
+        def turn_pooled(t, g):
+            pooled_t[t, g] = psum.tile([P, PACK, P], F32, tag="pT", bufs=4, name="pooled_t")
+            for i in range(PACK):
                 for term in range(TERMS):
                     nc.tensor.matmul(
                         pooled_t[t, g][:, i, :],
@@ -228,12 +230,9 @@ def tile_rarevariantawarefusion_pa_kernel(
                 in_=grouped[t][:].rearrange("p g r i -> p (g r i)"),
             )
 
-        def multiply(t, chunk):
-            n = chunk * N_HALVES // CHUNKS
-            per_chunk = N_HALVES * PASSES // CHUNKS
-            if chunk * N_HALVES % CHUNKS == 0:
-                acc[t, n] = psum.tile([P, N_TILE], F32, tag="acc", name="acc")
-            for g in range(chunk * per_chunk % PASSES, chunk * per_chunk % PASSES + per_chunk):
+        def multiply(t, n):
+            acc[t, n] = psum.tile([P, N_TILE], F32, tag="acc", name="acc")
+            for g in range(PASSES):
                 nc.tensor.matmul_mx(
                     out=acc[t, n][:],
                     lhsT=x_codes[t][:, g * P : (g + 1) * P].bitcast(FP8X4),
@@ -304,47 +303,47 @@ def tile_rarevariantawarefusion_pa_kernel(
             )
             nc.sync.dma_start(out=out[t // J].rearrange("(p j) d -> p j d", j=J)[:, t % J, :], in_=res[:])
 
-        def tensor_chunk(turning, multiplying, chunk):
-            if live(turning):
-                if chunk == 0:
-                    turn_orig(turning)
-                turn_pooled(turning, chunk)
+        def tensor_half(turning, multiplying, h):
             if live(multiplying):
-                multiply(multiplying, chunk)
+                multiply(multiplying, h)
+            if live(turning):
+                if h == 0:
+                    turn_orig(turning)
+                turn_pooled(turning, h)
 
         for step in range(TILES + 3):
             widening, turning, multiplying, norming = step, step - 1, step - 2, step - 3
-            if live(multiplying):
-                copy_out_pooled(multiplying, 1)
-                quantise(multiplying)
             if live(norming):
                 variance(norming)
             if live(widening):
+                sum_rest(widening)
                 max_tree(widening)
                 widen(widening, 0, 4)
             if live(norming):
                 affine(norming)
-            tensor_chunk(turning, multiplying, 0)
-            tensor_chunk(turning, multiplying, 1)
+            tensor_half(turning, multiplying, 0)
             if live(multiplying):
                 add_bias(multiplying, 0)
             if live(norming):
                 gelu(norming)
             if live(widening):
-                widen(widening, 4, TERMS)
+                widen_rest(widening)
+                widen(widening, 4, SCALAR_TERMS)
             if live(norming):
                 residual(norming)
             if live(widening + RAG_BUFS):
                 load_refs(widening + RAG_BUFS)
                 if (widening + RAG_BUFS) % J == 0:
                     load_orig((widening + RAG_BUFS) // J)
-            tensor_chunk(turning, multiplying, 2)
-            tensor_chunk(turning, multiplying, 3)
-            if live(turning):
-                copy_out_orig(turning)
-                copy_out_pooled(turning, 0)
+            tensor_half(turning, multiplying, 1)
             if live(multiplying):
                 add_bias(multiplying, 1)
                 mean(multiplying)
-            for t in range(GATES_AHEAD + 2 * step, min(GATES_AHEAD + 2 * step + 2, TILES)):
-                gate(t)
+            if live(turning):
+                copy_out_orig(turning)
+                copy_out_pooled(turning, 0)
+                copy_out_pooled(turning, 1)
+                quantise(turning)
+            if GATES_AHEAD + 2 * step < TILES:
+                gate(GATES_AHEAD + 2 * step)
+                gate(GATES_AHEAD + 2 * step + 1)

@@ -26,8 +26,8 @@ N_TILE = 512
 N_HALVES = D // N_TILE
 LN_EPS = 1e-5
 MEAN_W, MAX_W = 0.7, 0.3
-SCALAR_TERMS = 6
-TERMS = SCALAR_TERMS + 1
+LONE_TERMS = 6
+TERMS = LONE_TERMS + 1
 RAG_BUFS = 4
 GATES_AHEAD = 4
 
@@ -125,7 +125,7 @@ def tile_rarevariantawarefusion_pa_kernel(
         s_all = const.tile([P, TILES], F32)
 
         def gate(t):
-            logits = work.tile([P, D], F32, tag="y")
+            logits = work.tile([P, D], F32)
             for n in range(N_HALVES):
                 cols = slice(n * N_TILE, (n + 1) * N_TILE)
                 z_ps = psum.tile([P, N_TILE], F32, tag="acc")
@@ -151,28 +151,19 @@ def tile_rarevariantawarefusion_pa_kernel(
         def sum_rest(t):
             rest[t] = work.tile([P, D], F32, name="rest")
             nc.vector.tensor_tensor(
-                out=rest[t][:], in0=refs[t][:, SCALAR_TERMS, :], in1=refs[t][:, SCALAR_TERMS + 1, :], op=ALU.add
+                out=rest[t][:], in0=refs[t][:, LONE_TERMS, :], in1=refs[t][:, LONE_TERMS + 1, :], op=ALU.add
             )
 
-        def max_tree(t):
-            r_t = refs[t]
-            m4 = work.tile([P, 4, D], BF16)
-            nc.vector.tensor_tensor(out=m4[:], in0=r_t[:, 0:4], in1=r_t[:, 4:8], op=ALU.max)
+        def max_of_halves(t):
+            maxima[t] = work.tile([P, 4, D], BF16, name="maxima")
+            nc.vector.tensor_tensor(out=maxima[t][:], in0=refs[t][:, 0:4], in1=refs[t][:, 4:8], op=ALU.max)
+
+        def max_of_four(t):
+            m4 = maxima[t]
             nc.vector.tensor_tensor(out=m4[:, 0:2], in0=m4[:, 0:2], in1=m4[:, 2:4], op=ALU.max)
             nc.vector.tensor_tensor(out=m4[:, 0], in0=m4[:, 0], in1=m4[:, 1], op=ALU.max)
-            maxima[t] = m4
-            wide[t] = terms.tile([P, TERMS, HALF_PASSES, PACK, P], F32, name="wide")
 
-        def by_word(row):
-            return row.rearrange("p (g q i) -> p g i q", g=HALF_PASSES, i=PACK)
-
-        def widen(t, first, last):
-            for k in range(first, last):
-                nc.scalar.activation(
-                    out=wide[t][:, k], in_=by_word(refs[t][:, k, :]), func=ACT.Copy, scale=s_all[:, t : t + 1]
-                )
-
-        def widen_rest(t):
+        def add_max(t):
             nc.vector.scalar_tensor_tensor(
                 out=rest[t][:],
                 in0=maxima[t][:, 0, :],
@@ -181,7 +172,18 @@ def tile_rarevariantawarefusion_pa_kernel(
                 op0=ALU.mult,
                 op1=ALU.add,
             )
-            nc.vector.tensor_scalar_mul(out=wide[t][:, SCALAR_TERMS], in0=by_word(rest[t][:]), scalar1=s_all[:, t : t + 1])
+
+        def widen(t, first, last):
+            if first == 0:
+                wide[t] = terms.tile([P, TERMS, HALF_PASSES, PACK, P], F32, name="wide")
+            for term in range(first, last):
+                row = refs[t][:, term, :] if term < LONE_TERMS else rest[t][:]
+                nc.scalar.activation(
+                    out=wide[t][:, term],
+                    in_=row.rearrange("p (g q i) -> p g i q", g=HALF_PASSES, i=PACK),
+                    func=ACT.Copy,
+                    scale=s_all[:, t : t + 1],
+                )
 
         def turn_orig(t):
             o_words = orig_sb[t // J][:, t % J, :].bitcast(F32)
@@ -190,18 +192,20 @@ def tile_rarevariantawarefusion_pa_kernel(
                 for u in range(2):
                     nc.tensor.transpose(orig_t[t][:, g, u, :], o_words[:, 256 * g + u : 256 * (g + 1) : 2], ident_f32[:])
 
-        def turn_pooled(t, g):
-            pooled_t[t, g] = psum.tile([P, PACK, P], F32, tag="pT", bufs=4, name="pooled_t")
-            for i in range(PACK):
-                for term in range(TERMS):
-                    nc.tensor.matmul(
-                        pooled_t[t, g][:, i, :],
-                        lhsT=wide[t][:, term, g, i, :],
-                        rhs=ident_f32[:],
-                        is_transpose=True,
-                        start=(term == 0),
-                        stop=(term == TERMS - 1),
-                    )
+        def turn(t, first, last):
+            for term in range(first, last):
+                for g in range(HALF_PASSES):
+                    if term == 0:
+                        pooled_t[t, g] = psum.tile([P, PACK, P], F32, tag="pT", bufs=4, name="pooled_t")
+                    for i in range(PACK):
+                        nc.tensor.matmul(
+                            pooled_t[t, g][:, i, :],
+                            lhsT=wide[t][:, term, g, i, :],
+                            rhs=ident_f32[:],
+                            is_transpose=True,
+                            start=(term == 0 and i == 0),
+                            stop=(term == TERMS - 1 and i == PACK - 1),
+                        )
 
         def copy_out_orig(t):
             grouped[t] = work.tile([P, PASSES, P, PACK], BF16, align_bytes=64, name="grouped")
@@ -303,47 +307,48 @@ def tile_rarevariantawarefusion_pa_kernel(
             )
             nc.sync.dma_start(out=out[t // J].rearrange("(p j) d -> p j d", j=J)[:, t % J, :], in_=res[:])
 
-        def tensor_half(turning, multiplying, h):
-            if live(multiplying):
-                multiply(multiplying, h)
-            if live(turning):
-                if h == 0:
-                    turn_orig(turning)
-                turn_pooled(turning, h)
-
-        for step in range(TILES + 3):
-            widening, turning, multiplying, norming = step, step - 1, step - 2, step - 3
+        for step in range(TILES + 2):
+            pooling, multiplying, norming = step, step - 1, step - 2
             if live(norming):
                 variance(norming)
-            if live(widening):
-                sum_rest(widening)
-                max_tree(widening)
-                widen(widening, 0, 4)
+            if live(pooling):
+                sum_rest(pooling)
+                max_of_halves(pooling)
+                widen(pooling, 0, 2)
+            if live(multiplying):
+                turn(multiplying, 4, TERMS)
+            if live(pooling):
+                turn_orig(pooling)
+                turn(pooling, 0, 2)
+            if live(multiplying):
+                copy_out_orig(multiplying)
+                copy_out_pooled(multiplying, 0)
+                copy_out_pooled(multiplying, 1)
             if live(norming):
                 affine(norming)
-            tensor_half(turning, multiplying, 0)
             if live(multiplying):
-                add_bias(multiplying, 0)
+                quantise(multiplying)
+                multiply(multiplying, 0)
+                multiply(multiplying, 1)
+            if live(pooling):
+                max_of_four(pooling)
+                widen(pooling, 2, 4)
+                turn(pooling, 2, 4)
             if live(norming):
                 gelu(norming)
-            if live(widening):
-                widen_rest(widening)
-                widen(widening, 4, SCALAR_TERMS)
+            if live(pooling):
+                add_max(pooling)
+                widen(pooling, 4, TERMS)
             if live(norming):
                 residual(norming)
-            if live(widening + RAG_BUFS):
-                load_refs(widening + RAG_BUFS)
-                if (widening + RAG_BUFS) % J == 0:
-                    load_orig((widening + RAG_BUFS) // J)
-            tensor_half(turning, multiplying, 1)
+            if live(pooling + RAG_BUFS):
+                load_refs(pooling + RAG_BUFS)
+                if (pooling + RAG_BUFS) % J == 0:
+                    load_orig((pooling + RAG_BUFS) // J)
             if live(multiplying):
+                add_bias(multiplying, 0)
                 add_bias(multiplying, 1)
                 mean(multiplying)
-            if live(turning):
-                copy_out_orig(turning)
-                copy_out_pooled(turning, 0)
-                copy_out_pooled(turning, 1)
-                quantise(turning)
             if GATES_AHEAD + 2 * step < TILES:
                 gate(GATES_AHEAD + 2 * step)
                 gate(GATES_AHEAD + 2 * step + 1)

@@ -28,6 +28,7 @@ LN_EPS = 1e-5
 MEAN_W, MAX_W = 0.7, 0.3
 LONE_TERMS = 6
 TERMS = LONE_TERMS + 1
+LINE = 4
 RAG_BUFS = 4
 GATES_AHEAD = 4
 
@@ -175,12 +176,12 @@ def tile_rarevariantawarefusion_pa_kernel(
 
         def widen(t, first, last):
             if first == 0:
-                wide[t] = terms.tile([P, TERMS, HALF_PASSES, PACK, P], F32, name="wide")
+                wide[t] = terms.tile([P, TERMS, PACK, HALF_PASSES, P], F32, name="wide")
             for term in range(first, last):
                 row = refs[t][:, term, :] if term < LONE_TERMS else rest[t][:]
                 nc.scalar.activation(
-                    out=wide[t][:, term],
-                    in_=row.rearrange("p (g q i) -> p g i q", g=HALF_PASSES, i=PACK),
+                    out=wide[t][:, term].rearrange("p i g (c j) -> p (g c) i j", j=LINE),
+                    in_=row.rearrange("p (c j i) -> p c i j", j=LINE, i=PACK),
                     func=ACT.Copy,
                     scale=s_all[:, t : t + 1],
                 )
@@ -200,7 +201,7 @@ def tile_rarevariantawarefusion_pa_kernel(
                     for i in range(PACK):
                         nc.tensor.matmul(
                             pooled_t[t, g][:, i, :],
-                            lhsT=wide[t][:, term, g, i, :],
+                            lhsT=wide[t][:, term, i, g, :],
                             rhs=ident_f32[:],
                             is_transpose=True,
                             start=(term == 0 and i == 0),

@@ -216,7 +216,7 @@ def tile_rarevariantawarefusion_pa_kernel(
                 .bitcast(F32)
                 .rearrange("p (g r u) -> p g r u", g=HALF_PASSES, u=2)
             )
-            nc.scalar.copy(out=o_grouped, in_=orig_t[t][:].rearrange("p g u r -> p g r u"))
+            nc.vector.tensor_copy(out=o_grouped, in_=orig_t[t][:].rearrange("p g u r -> p g r u"))
 
         def copy_out_pooled(t, g):
             nc.scalar.activation(
@@ -350,6 +350,6 @@ def tile_rarevariantawarefusion_pa_kernel(
                 add_bias(multiplying, 0)
                 add_bias(multiplying, 1)
                 mean(multiplying)
-            if GATES_AHEAD + 2 * step < TILES:
-                gate(GATES_AHEAD + 2 * step)
-                gate(GATES_AHEAD + 2 * step + 1)
+            if step == 0:
+                for t in range(GATES_AHEAD, TILES):
+                    gate(t)

@@ -26,11 +26,12 @@ N_TILE = 512
 N_HALVES = D // N_TILE
 LN_EPS = 1e-5
 MEAN_W, MAX_W = 0.7, 0.3
-LONE_TERMS = 6
-TERMS = LONE_TERMS + 1
+MAXIMUM = REFS
+TERMS = REFS + 1
 LINE = 4
+GATES_ON_VECTOR = 2
+GATES_AHEAD = 5
 RAG_BUFS = 4
-GATES_AHEAD = 4
 
 FLOPS = 2 * B * L * (2 * D) * D + 2 * B * L * H * D
 
@@ -48,8 +49,8 @@ def tile_rarevariantawarefusion_pa_kernel(
         psum = ctx.enter_context(tc.psum_pool(name="psum", bufs=2))
         ctx.enter_context(tc.manual_schedule())
 
-        orig_sb, refs, rest, maxima, wide, orig_t, pooled_t, grouped = {}, {}, {}, {}, {}, {}, {}, {}
-        x_codes, x_planes, acc, y, y_sum, neg_mean, rstd = {}, {}, {}, {}, {}, {}, {}
+        orig_sb, refs, maxima, wide, turned, orig_t, pooled_t, grouped = {}, {}, {}, {}, {}, {}, {}, {}
+        x_codes, x_planes, acc, y, y_sum, neg_mean, rstd, res = {}, {}, {}, {}, {}, {}, {}, {}
 
         def live(t):
             return 0 <= t < TILES
@@ -123,23 +124,44 @@ def tile_rarevariantawarefusion_pa_kernel(
         hT = const.tile([P, TILES, P], BF16)
         nc.vector.tensor_copy(out=hT[:], in_=hT_ps[:])
         b2_bc = spread(0)
+        s_parts = const.tile([P, N_HALVES, TILES], F32)
         s_all = const.tile([P, TILES], F32)
+        first_row = const.tile([P, P], BF16)
+        nc.vector.memset(first_row[:], 0.0)
+        nc.vector.memset(first_row[0:1, :], 1.0)
 
         def gate(t):
-            logits = work.tile([P, D], F32)
+            on_vector = t < GATES_ON_VECTOR
             for n in range(N_HALVES):
-                cols = slice(n * N_TILE, (n + 1) * N_TILE)
                 z_ps = psum.tile([P, N_TILE], F32, tag="acc")
-                nc.tensor.matmul(z_ps[:], lhsT=hT[:, t, :], rhs=w2_sb[:, cols], start=True, stop=True)
-                nc.vector.tensor_tensor(out=logits[:, cols], in0=z_ps[:], in1=b2_bc[:, cols], op=ALU.add)
-            gates = work.tile([P, D], BF16, tag="unread")
-            nc.scalar.activation(out=gates[:], in_=logits[:], func=ACT.Sigmoid, accum_out=s_all[:, t : t + 1])
+                cols = slice(n * N_TILE, (n + 1) * N_TILE)
+                nc.tensor.matmul(z_ps[:], lhsT=hT[:, t, :], rhs=w2_sb[:, cols], start=True, stop=on_vector)
+                logits = z_ps
+                if on_vector:
+                    logits = work.tile([P, N_TILE], F32, name="logits")
+                    nc.vector.tensor_tensor(out=logits[:], in0=z_ps[:], in1=b2_bc[:, cols], op=ALU.add)
+                else:
+                    nc.tensor.matmul(z_ps[:], lhsT=first_row[:], rhs=b2_bc[:, cols], start=False, stop=True)
+                gates = work.tile([P, N_TILE], BF16, name="gates")
+                nc.scalar.activation(
+                    out=gates[:], in_=logits[:], func=ACT.Sigmoid, accum_out=s_parts[:, n, t : t + 1]
+                )
 
-        for t in range(GATES_AHEAD):
+        s_max = const.tile([P, TILES], F32)
+
+        def sum_gates(first, last):
+            nc.vector.tensor_tensor(
+                out=s_all[:, first:last], in0=s_parts[:, 0, first:last], in1=s_parts[:, 1, first:last], op=ALU.add
+            )
+            nc.vector.tensor_scalar_mul(out=s_max[:, first:last], in0=s_all[:, first:last], scalar1=MAX_W * REFS / MEAN_W)
+
+        for t in range(GATES_ON_VECTOR):
             gate(t)
         biasf_bc = spread(1)
         lng_bc = spread(2)
         lnb_bc = spread(3)
+        for t in range(GATES_ON_VECTOR, GATES_AHEAD):
+            gate(t)
 
         af_flat = af_sb[:].rearrange("p b j -> p (b j)")
         one_minus = const.tile([P, TILES], F32)
@@ -148,12 +170,6 @@ def tile_rarevariantawarefusion_pa_kernel(
         nc.vector.tensor_tensor(out=spread_af[:], in0=one_minus[:], in1=af_flat, op=ALU.mult)
         af_scale = const.tile([P, TILES], F32)
         nc.gpsimd.tensor_tensor(out=af_scale[:], in0=spread_af[:], in1=half[:], op=ALU.pow)
-
-        def sum_rest(t):
-            rest[t] = work.tile([P, D], F32, name="rest")
-            nc.vector.tensor_tensor(
-                out=rest[t][:], in0=refs[t][:, LONE_TERMS, :], in1=refs[t][:, LONE_TERMS + 1, :], op=ALU.add
-            )
 
         def max_of_halves(t):
             maxima[t] = work.tile([P, 4, D], BF16, name="maxima")
@@ -164,27 +180,17 @@ def tile_rarevariantawarefusion_pa_kernel(
             nc.vector.tensor_tensor(out=m4[:, 0:2], in0=m4[:, 0:2], in1=m4[:, 2:4], op=ALU.max)
             nc.vector.tensor_tensor(out=m4[:, 0], in0=m4[:, 0], in1=m4[:, 1], op=ALU.max)
 
-        def add_max(t):
-            nc.vector.scalar_tensor_tensor(
-                out=rest[t][:],
-                in0=maxima[t][:, 0, :],
-                scalar=MAX_W * REFS / MEAN_W,
-                in1=rest[t][:],
-                op0=ALU.mult,
-                op1=ALU.add,
-            )
-
-        def widen(t, first, last):
-            if first == 0:
+        def widen(t, term, on_vector):
+            if t not in wide:
                 wide[t] = terms.tile([P, TERMS, PACK, HALF_PASSES, P], F32, name="wide")
-            for term in range(first, last):
-                row = refs[t][:, term, :] if term < LONE_TERMS else rest[t][:]
-                nc.scalar.activation(
-                    out=wide[t][:, term].rearrange("p i g (c j) -> p (g c) i j", j=LINE),
-                    in_=row.rearrange("p (c j i) -> p c i j", j=LINE, i=PACK),
-                    func=ACT.Copy,
-                    scale=s_all[:, t : t + 1],
-                )
+            row = maxima[t][:, 0, :] if term == MAXIMUM else refs[t][:, term, :]
+            factor = (s_max if term == MAXIMUM else s_all)[:, t : t + 1]
+            out_view = wide[t][:, term].rearrange("p i g (c j) -> p (g c) i j", j=LINE)
+            in_view = row.rearrange("p (c j i) -> p c i j", j=LINE, i=PACK)
+            if on_vector:
+                nc.vector.tensor_scalar_mul(out=out_view, in0=in_view, scalar1=factor)
+            else:
+                nc.scalar.activation(out=out_view, in_=in_view, func=ACT.Copy, scale=factor)
 
         def turn_orig(t):
             o_words = orig_sb[t // J][:, t % J, :].bitcast(F32)
@@ -193,20 +199,20 @@ def tile_rarevariantawarefusion_pa_kernel(
                 for u in range(2):
                     nc.tensor.transpose(orig_t[t][:, g, u, :], o_words[:, 256 * g + u : 256 * (g + 1) : 2], ident_f32[:])
 
-        def turn(t, first, last):
-            for term in range(first, last):
-                for g in range(HALF_PASSES):
-                    if term == 0:
-                        pooled_t[t, g] = psum.tile([P, PACK, P], F32, tag="pT", bufs=4, name="pooled_t")
-                    for i in range(PACK):
-                        nc.tensor.matmul(
-                            pooled_t[t, g][:, i, :],
-                            lhsT=wide[t][:, term, i, g, :],
-                            rhs=ident_f32[:],
-                            is_transpose=True,
-                            start=(term == 0 and i == 0),
-                            stop=(term == TERMS - 1 and i == PACK - 1),
-                        )
+        def turn(t, term):
+            turned[t] = turned.get(t, 0) + 1
+            for g in range(HALF_PASSES):
+                if turned[t] == 1:
+                    pooled_t[t, g] = psum.tile([P, PACK, P], F32, tag="pT", bufs=4, name="pooled_t")
+                for i in range(PACK):
+                    nc.tensor.matmul(
+                        pooled_t[t, g][:, i, :],
+                        lhsT=wide[t][:, term, i, g, :],
+                        rhs=ident_f32[:],
+                        is_transpose=True,
+                        start=(turned[t] == 1 and i == 0),
+                        stop=(turned[t] == TERMS and i == PACK - 1),
+                    )
 
         def copy_out_orig(t):
             grouped[t] = work.tile([P, PASSES, P, PACK], BF16, align_bytes=64, name="grouped")
@@ -218,26 +224,29 @@ def tile_rarevariantawarefusion_pa_kernel(
             )
             nc.vector.tensor_copy(out=o_grouped, in_=orig_t[t][:].rearrange("p g u r -> p g r u"))
 
-        def copy_out_pooled(t, g):
-            nc.scalar.activation(
-                out=grouped[t][:, HALF_PASSES + g],
-                in_=pooled_t[t, g][:].rearrange("p i r -> p r i"),
-                func=ACT.Copy,
-                scale=MEAN_W / REFS,
-            )
+        def copy_out_pooled(t, g, on_vector=False):
+            out_view = grouped[t][:, HALF_PASSES + g]
+            in_view = pooled_t[t, g][:].rearrange("p i r -> p r i")
+            if on_vector:
+                nc.vector.tensor_scalar_mul(out=out_view, in0=in_view, scalar1=MEAN_W / REFS)
+            else:
+                nc.scalar.activation(out=out_view, in_=in_view, func=ACT.Copy, scale=MEAN_W / REFS)
 
-        def quantise(t):
-            x_codes[t] = work.tile([P, PASSES * P], U32, align_bytes=64, name="x_codes")
-            x_planes[t] = work.tile([P, PASSES * P], U8, align_bytes=64, name="x_planes")
+        def quantise(t, first, last):
+            if first == 0:
+                x_codes[t] = work.tile([P, PASSES * P], U32, align_bytes=64, name="x_codes")
+                x_planes[t] = work.tile([P, PASSES * P], U8, align_bytes=64, name="x_planes")
+            words = slice(first * P, last * P)
             nc.vector.quantize_mx(
-                out=x_codes[t][:].bitcast(FP8X4),
-                scales=x_planes[t][:],
-                in_=grouped[t][:].rearrange("p g r i -> p (g r i)"),
+                out=x_codes[t][:, words].bitcast(FP8X4),
+                scales=x_planes[t][:, words],
+                in_=grouped[t][:, first:last].rearrange("p g r i -> p (g r i)"),
             )
 
-        def multiply(t, n):
-            acc[t, n] = psum.tile([P, N_TILE], F32, tag="acc", name="acc")
-            for g in range(PASSES):
+        def multiply(t, n, first, last):
+            if first == 0:
+                acc[t, n] = psum.tile([P, N_TILE], F32, tag="acc", name="acc")
+            for g in range(first, last):
                 nc.tensor.matmul_mx(
                     out=acc[t, n][:],
                     lhsT=x_codes[t][:, g * P : (g + 1) * P].bitcast(FP8X4),
@@ -265,7 +274,8 @@ def tile_rarevariantawarefusion_pa_kernel(
 
         def mean(t):
             neg_mean[t] = work.tile([P, 1], F32, name="neg_mean")
-            nc.vector.tensor_scalar(
+            engine = nc.vector if t == TILES - 1 else nc.gpsimd
+            engine.tensor_scalar(
                 out=neg_mean[t][:],
                 in0=y_sum[t][:, 0:1],
                 scalar1=y_sum[t][:, 1:2],
@@ -285,71 +295,130 @@ def tile_rarevariantawarefusion_pa_kernel(
             rstd[t] = work.tile([P, 1], F32, name="rstd")
             nc.gpsimd.tensor_tensor(out=rstd[t][:], in0=var_eps[:], in1=neg_half[:], op=ALU.pow)
 
-        def affine(t):
+        def centre(t, cols):
             nc.vector.scalar_tensor_tensor(
-                out=y[t][:], in0=y[t][:], scalar=neg_mean[t][:], in1=lng_bc[:], op0=ALU.add, op1=ALU.mult
-            )
-            nc.vector.scalar_tensor_tensor(
-                out=y[t][:], in0=y[t][:], scalar=rstd[t][:], in1=lnb_bc[:], op0=ALU.mult, op1=ALU.add
+                out=y[t][:, cols], in0=y[t][:, cols], scalar=neg_mean[t][:], in1=lng_bc[:, cols], op0=ALU.add, op1=ALU.mult
             )
 
-        def gelu(t):
-            nc.scalar.activation(out=y[t][:], in_=y[t][:], func=ACT.Gelu)
-
-        def residual(t):
-            res = work.tile([P, D], F32)
+        def normalise(t, cols):
             nc.vector.scalar_tensor_tensor(
-                out=res[:],
-                in0=y[t][:],
+                out=y[t][:, cols], in0=y[t][:, cols], scalar=rstd[t][:], in1=lnb_bc[:, cols], op0=ALU.mult, op1=ALU.add
+            )
+
+        def gelu(t, cols):
+            nc.scalar.activation(out=y[t][:, cols], in_=y[t][:, cols], func=ACT.Gelu)
+
+        def residual(t, cols):
+            if cols.start == 0:
+                res[t] = work.tile([P, D], F32, name="res")
+            nc.vector.scalar_tensor_tensor(
+                out=res[t][:, cols],
+                in0=y[t][:, cols],
                 scalar=af_scale[:, t : t + 1],
-                in1=orig_sb[t // J][:, t % J, :],
+                in1=orig_sb[t // J][:, t % J, cols],
                 op0=ALU.mult,
                 op1=ALU.add,
             )
-            nc.sync.dma_start(out=out[t // J].rearrange("(p j) d -> p j d", j=J)[:, t % J, :], in_=res[:])
+            nc.sync.dma_start(
+                out=out[t // J].rearrange("(p j) d -> p j d", j=J)[:, t % J, cols], in_=res[t][:, cols]
+            )
 
-        for step in range(TILES + 2):
+        whole = slice(0, D)
+        halves = [slice(n * N_TILE, (n + 1) * N_TILE) for n in range(N_HALVES)]
+        last = TILES - 1
+        for step in range(TILES + 1):
             pooling, multiplying, norming = step, step - 1, step - 2
-            if live(norming):
-                variance(norming)
-            if live(pooling):
-                sum_rest(pooling)
-                max_of_halves(pooling)
-                widen(pooling, 0, 2)
-            if live(multiplying):
-                turn(multiplying, 4, TERMS)
-            if live(pooling):
-                turn_orig(pooling)
-                turn(pooling, 0, 2)
-            if live(multiplying):
-                copy_out_orig(multiplying)
-                copy_out_pooled(multiplying, 0)
-                copy_out_pooled(multiplying, 1)
-            if live(norming):
-                affine(norming)
-            if live(multiplying):
-                quantise(multiplying)
-                multiply(multiplying, 0)
-                multiply(multiplying, 1)
-            if live(pooling):
-                max_of_four(pooling)
-                widen(pooling, 2, 4)
-                turn(pooling, 2, 4)
-            if live(norming):
-                gelu(norming)
-            if live(pooling):
-                add_max(pooling)
-                widen(pooling, 4, TERMS)
-            if live(norming):
-                residual(norming)
+            mult, norm = live(multiplying), live(norming)
+            vector_terms = list({0: range(8), 1: range(4, 8)}.get(step, range(6, 8)))
+            scalar_terms = [k for k in range(REFS) if k not in vector_terms]
+            early = vector_terms[: max(0, len(vector_terms) - 4)]
+            late = vector_terms[len(early) :]
+
+            def on_scalar(count):
+                for k in scalar_terms[:count]:
+                    widen(pooling, k, False)
+                    turn(pooling, k)
+                scalar_terms[:count] = []
+
+            if multiplying == last:
+                centre(norming, whole)
+                quantise(last, 0, HALF_PASSES)
+                for n in range(N_HALVES):
+                    multiply(last, n, 0, HALF_PASSES)
+                copy_out_pooled(last, 0)
+                copy_out_pooled(last, 1, True)
+                for g in range(HALF_PASSES, PASSES):
+                    quantise(last, g, g + 1)
+                    for n in range(N_HALVES):
+                        multiply(last, n, g, g + 1)
+                normalise(norming, whole)
+                gelu(norming, whole)
+                for n in range(N_HALVES):
+                    add_bias(last, n)
+                mean(last)
+                variance(last)
+                residual(norming, whole)
+                for cols in halves:
+                    centre(last, cols)
+                for cols in halves:
+                    normalise(last, cols)
+                    gelu(last, cols)
+                for cols in halves:
+                    residual(last, cols)
+                continue
+
+            max_of_halves(pooling)
+            if step == 0:
+                sum_gates(0, GATES_ON_VECTOR)
+            for k in early:
+                widen(pooling, k, True)
+                turn(pooling, k)
+            on_scalar(1)
+            if norm:
+                for g in range(HALF_PASSES):
+                    copy_out_pooled(multiplying, g)
+                centre(norming, whole)
+                normalise(norming, whole)
+            on_scalar(2)
+            if norm:
+                quantise(multiplying, 0, PASSES)
+                for n in range(N_HALVES):
+                    multiply(multiplying, n, 0, PASSES)
+            max_of_four(pooling)
+            if norm:
+                gelu(norming, whole)
+            if step == 0:
+                sum_gates(GATES_ON_VECTOR, GATES_AHEAD)
+                for t in range(GATES_AHEAD, TILES):
+                    gate(t)
+            on_scalar(1)
+            turn_orig(pooling)
+            for k in late[:-1]:
+                widen(pooling, k, True)
+                turn(pooling, k)
+            if mult and not norm:
+                for g in range(HALF_PASSES):
+                    copy_out_pooled(multiplying, g)
+                quantise(multiplying, 0, PASSES)
+                for n in range(N_HALVES):
+                    multiply(multiplying, n, 0, PASSES)
+                sum_gates(GATES_AHEAD, TILES)
+            widen(pooling, MAXIMUM, False)
+            turn(pooling, MAXIMUM)
+            if mult:
+                for n in range(N_HALVES):
+                    add_bias(multiplying, n)
+                mean(multiplying)
+            on_scalar(1)
+            widen(pooling, late[-1], True)
+            turn(pooling, late[-1])
+            if norm:
+                residual(norming, whole)
+            if mult:
+                variance(multiplying)
+            copy_out_orig(pooling)
+            on_scalar(1)
             if live(pooling + RAG_BUFS):
                 load_refs(pooling + RAG_BUFS)
                 if (pooling + RAG_BUFS) % J == 0:
                     load_orig((pooling + RAG_BUFS) // J)
-            if live(multiplying):
-                add_bias(multiplying, 0)
-                add_bias(multiplying, 1)
-                mean(multiplying)
-            if step == 0:
-                for t in range(GATES_AHEAD, TILES):
-                    gate(t)

@@ -274,8 +274,7 @@ def tile_rarevariantawarefusion_pa_kernel(
 
         def mean(t):
             neg_mean[t] = work.tile([P, 1], F32, name="neg_mean")
-            engine = nc.vector if t == TILES - 1 else nc.gpsimd
-            engine.tensor_scalar(
+            nc.vector.tensor_scalar(
                 out=neg_mean[t][:],
                 in0=y_sum[t][:, 0:1],
                 scalar1=y_sum[t][:, 1:2],
@@ -408,10 +407,11 @@ def tile_rarevariantawarefusion_pa_kernel(
             if mult:
                 for n in range(N_HALVES):
                     add_bias(multiplying, n)
-                mean(multiplying)
             on_scalar(1)
             widen(pooling, late[-1], True)
             turn(pooling, late[-1])
+            if mult:
+                mean(multiplying)
             if norm:
                 residual(norming, whole)
             if mult:

@@ -328,7 +328,7 @@ def tile_rarevariantawarefusion_pa_kernel(
         for step in range(TILES + 1):
             pooling, multiplying, norming = step, step - 1, step - 2
             mult, norm = live(multiplying), live(norming)
-            vector_terms = list({0: range(8), 1: range(4, 8)}.get(step, range(6, 8)))
+            vector_terms = list({0: range(8), 1: range(4, 8)}.get(step, range(5, 8)))
             scalar_terms = [k for k in range(REFS) if k not in vector_terms]
             early = vector_terms[: max(0, len(vector_terms) - 4)]
             late = vector_terms[len(early) :]

@@ -29,8 +29,7 @@ MEAN_W, MAX_W = 0.7, 0.3
 MAXIMUM = REFS
 TERMS = REFS + 1
 LINE = 4
-GATES_ON_VECTOR = 2
-GATES_AHEAD = 5
+GATES_BY_TRANSPOSES = 2
 RAG_BUFS = 4
 
 FLOPS = 2 * B * L * (2 * D) * D + 2 * B * L * H * D
@@ -103,48 +102,68 @@ def tile_rarevariantawarefusion_pa_kernel(
         nc.vector.memset(half[:], 0.5)
         neg_half = const.tile([P, 1], F32)
         nc.vector.memset(neg_half[:], -0.5)
+        first_row = const.tile([P, P], BF16)
+        nc.vector.memset(first_row[:], 0.0)
+        nc.vector.memset(first_row[0:1, :], 1.0)
+        first_table = const.tile([P, 1], F32)
+        nc.scalar.activation(out=first_table[:], in_=neg_half[:], func=ACT.Sigmoid)
 
         cols_ps = psum.tile([P, P], BF16, tag="oT")
         nc.tensor.transpose(cols_ps[:], vec_rows[:], ident_bf[:])
         vec_cols = const.tile([P, 4 * BLOCKS], BF16)
         nc.vector.tensor_copy(out=vec_cols[:], in_=cols_ps[:, 0 : 4 * BLOCKS])
+        b2_cols = const.tile([P, BLOCKS], F32)
+        nc.vector.tensor_copy(out=b2_cols[:], in_=cols_ps[:, 0:BLOCKS])
 
-        def spread(v):
-            spread_ps = psum.tile([P, BLOCKS, P], BF16, tag="oT")
+        def turn_spread(v):
+            spread_ps = psum.tile([P, BLOCKS, P], BF16, tag="oT", name="spread_ps")
             for c in range(BLOCKS):
                 col = v * BLOCKS + c
                 nc.tensor.transpose(spread_ps[:, c, :], vec_cols[:, col : col + 1].to_broadcast([P, P]), ident_bf[:])
+            return spread_ps
+
+        def keep_spread(v, spread_ps):
             everywhere = const.tile([P, D], BF16, name="everywhere%d" % v)
             nc.vector.tensor_copy(out=everywhere[:], in_=spread_ps[:].rearrange("p c m -> p (c m)"))
             return everywhere
+
+        def spread(v):
+            return keep_spread(v, turn_spread(v))
 
         hT_ps = psum.tile([P, TILES, P], BF16, tag="oT")
         for t in range(TILES):
             nc.tensor.transpose(hT_ps[:, t, :], haf[:, t // J, t % J, :], ident_bf[:])
         hT = const.tile([P, TILES, P], BF16)
-        nc.vector.tensor_copy(out=hT[:], in_=hT_ps[:])
+        nc.scalar.copy(out=hT[:], in_=hT_ps[:])
         b2_bc = spread(0)
         s_parts = const.tile([P, N_HALVES, TILES], F32)
         s_all = const.tile([P, TILES], F32)
-        first_row = const.tile([P, P], BF16)
-        nc.vector.memset(first_row[:], 0.0)
-        nc.vector.memset(first_row[0:1, :], 1.0)
 
         def gate(t):
-            on_vector = t < GATES_ON_VECTOR
             for n in range(N_HALVES):
-                z_ps = psum.tile([P, N_TILE], F32, tag="acc")
+                if t % 3 < 2:
+                    z_ps = psum.tile([P, N_TILE], F32, tag="pT", bufs=4)
+                else:
+                    z_ps = psum.tile([P, N_TILE], F32, tag="acc")
                 cols = slice(n * N_TILE, (n + 1) * N_TILE)
-                nc.tensor.matmul(z_ps[:], lhsT=hT[:, t, :], rhs=w2_sb[:, cols], start=True, stop=on_vector)
-                logits = z_ps
-                if on_vector:
-                    logits = work.tile([P, N_TILE], F32, name="logits")
-                    nc.vector.tensor_tensor(out=logits[:], in0=z_ps[:], in1=b2_bc[:, cols], op=ALU.add)
+                nc.tensor.matmul(z_ps[:], lhsT=hT[:, t, :], rhs=w2_sb[:, cols], start=True, stop=False)
+                if t < GATES_BY_TRANSPOSES:
+                    chunks = N_TILE // P
+                    for c in range(chunks):
+                        col = n * chunks + c
+                        nc.tensor.matmul(
+                            z_ps[:, c * P : (c + 1) * P],
+                            lhsT=b2_cols[:, col : col + 1].to_broadcast([P, P]),
+                            rhs=ident_f32[:],
+                            is_transpose=True,
+                            start=False,
+                            stop=(c == chunks - 1),
+                        )
                 else:
                     nc.tensor.matmul(z_ps[:], lhsT=first_row[:], rhs=b2_bc[:, cols], start=False, stop=True)
                 gates = work.tile([P, N_TILE], BF16, name="gates")
                 nc.scalar.activation(
-                    out=gates[:], in_=logits[:], func=ACT.Sigmoid, accum_out=s_parts[:, n, t : t + 1]
+                    out=gates[:], in_=z_ps[:], func=ACT.Sigmoid, accum_out=s_parts[:, n, t : t + 1]
                 )
 
         s_max = const.tile([P, TILES], F32)
@@ -155,29 +174,35 @@ def tile_rarevariantawarefusion_pa_kernel(
             )
             nc.vector.tensor_scalar_mul(out=s_max[:, first:last], in0=s_all[:, first:last], scalar1=MAX_W * REFS / MEAN_W)
 
-        for t in range(GATES_ON_VECTOR):
-            gate(t)
-        biasf_bc = spread(1)
-        lng_bc = spread(2)
-        lnb_bc = spread(3)
-        for t in range(GATES_ON_VECTOR, GATES_AHEAD):
+        gate(0)
+        f_ps = turn_spread(1)
+        gate(1)
+        g_ps = turn_spread(2)
+        for t in range(2, TILES):
             gate(t)
 
-        af_flat = af_sb[:].rearrange("p b j -> p (b j)")
-        one_minus = const.tile([P, TILES], F32)
-        nc.vector.tensor_scalar(out=one_minus[:], in0=af_flat, scalar1=-1.0, scalar2=1.0, op0=ALU.mult, op1=ALU.add)
-        spread_af = const.tile([P, TILES], F32)
-        nc.vector.tensor_tensor(out=spread_af[:], in0=one_minus[:], in1=af_flat, op=ALU.mult)
-        af_scale = const.tile([P, TILES], F32)
-        nc.gpsimd.tensor_tensor(out=af_scale[:], in0=spread_af[:], in1=half[:], op=ALU.pow)
+        def spread_of_af():
+            af_flat = af_sb[:].rearrange("p b j -> p (b j)")
+            one_minus = const.tile([P, TILES], F32)
+            nc.vector.tensor_scalar(
+                out=one_minus[:], in0=af_flat, scalar1=-1.0, scalar2=1.0, op0=ALU.mult, op1=ALU.add
+            )
+            product = const.tile([P, TILES], F32)
+            nc.vector.tensor_tensor(out=product[:], in0=one_minus[:], in1=af_flat, op=ALU.mult)
+            root = const.tile([P, TILES], F32)
+            nc.gpsimd.tensor_tensor(out=root[:], in0=product[:], in1=half[:], op=ALU.pow)
+            return root
 
         def max_of_halves(t):
             maxima[t] = work.tile([P, 4, D], BF16, name="maxima")
             nc.vector.tensor_tensor(out=maxima[t][:], in0=refs[t][:, 0:4], in1=refs[t][:, 4:8], op=ALU.max)
 
-        def max_of_four(t):
+        def max_of_quarters(t):
             m4 = maxima[t]
             nc.vector.tensor_tensor(out=m4[:, 0:2], in0=m4[:, 0:2], in1=m4[:, 2:4], op=ALU.max)
+
+        def max_of_two(t):
+            m4 = maxima[t]
             nc.vector.tensor_tensor(out=m4[:, 0], in0=m4[:, 0], in1=m4[:, 1], op=ALU.max)
 
         def widen(t, term, on_vector):
@@ -325,100 +350,143 @@ def tile_rarevariantawarefusion_pa_kernel(
         whole = slice(0, D)
         halves = [slice(n * N_TILE, (n + 1) * N_TILE) for n in range(N_HALVES)]
         last = TILES - 1
-        for step in range(TILES + 1):
-            pooling, multiplying, norming = step, step - 1, step - 2
-            mult, norm = live(multiplying), live(norming)
-            vector_terms = list({0: range(8), 1: range(4, 8)}.get(step, range(5, 8)))
-            scalar_terms = [k for k in range(REFS) if k not in vector_terms]
-            early = vector_terms[: max(0, len(vector_terms) - 4)]
-            late = vector_terms[len(early) :]
 
-            def on_scalar(count):
-                for k in scalar_terms[:count]:
-                    widen(pooling, k, False)
-                    turn(pooling, k)
-                scalar_terms[:count] = []
+        def on_vector(t, terms):
+            for k in terms:
+                widen(t, k, True)
+                turn(t, k)
 
-            if multiplying == last:
-                centre(norming, whole)
-                quantise(last, 0, HALF_PASSES)
-                for n in range(N_HALVES):
-                    multiply(last, n, 0, HALF_PASSES)
-                copy_out_pooled(last, 0)
-                copy_out_pooled(last, 1, True)
-                for g in range(HALF_PASSES, PASSES):
-                    quantise(last, g, g + 1)
-                    for n in range(N_HALVES):
-                        multiply(last, n, g, g + 1)
-                normalise(norming, whole)
-                gelu(norming, whole)
-                for n in range(N_HALVES):
-                    add_bias(last, n)
-                mean(last)
-                variance(last)
-                residual(norming, whole)
-                for cols in halves:
-                    centre(last, cols)
-                for cols in halves:
-                    normalise(last, cols)
-                    gelu(last, cols)
-                for cols in halves:
-                    residual(last, cols)
-                continue
+        def on_scalar(t, terms):
+            for k in terms:
+                widen(t, k, False)
+                turn(t, k)
 
+        def copy_out(t):
+            for g in range(HALF_PASSES):
+                copy_out_pooled(t, g)
+
+        def quantise_and_multiply(t):
+            quantise(t, 0, PASSES)
+            for n in range(N_HALVES):
+                multiply(t, n, 0, PASSES)
+
+        def add_biases(t):
+            for n in range(N_HALVES):
+                add_bias(t, n)
+
+        def load(t):
+            if live(t):
+                load_refs(t)
+                if t % J == 0:
+                    load_orig(t // J)
+
+        max_of_halves(0)
+        sum_gates(0, 1)
+        biasf_bc = keep_spread(1, f_ps)
+        lng_bc = keep_spread(2, g_ps)
+        b_ps = turn_spread(3)
+        turn_orig(0)
+        on_vector(0, range(0, 3))
+        max_of_quarters(0)
+        on_vector(0, range(3, 4))
+        max_of_two(0)
+        on_vector(0, range(4, 6))
+        copy_out_orig(0)
+        on_scalar(0, [MAXIMUM])
+        on_scalar(0, range(6, 8))
+        sum_gates(1, TILES)
+        lnb_bc = keep_spread(3, b_ps)
+        af_scale = spread_of_af()
+        load(RAG_BUFS)
+
+        max_of_halves(1)
+        turn_orig(1)
+        on_scalar(1, range(0, 3))
+        max_of_quarters(1)
+        on_vector(1, range(5, 6))
+        max_of_two(1)
+        on_vector(1, range(6, 8))
+        on_scalar(1, [MAXIMUM])
+        copy_out(0)
+        copy_out_orig(1)
+        quantise_and_multiply(0)
+        on_scalar(1, range(3, 5))
+        load(1 + RAG_BUFS)
+
+        max_of_halves(2)
+        on_scalar(2, range(0, 2))
+        turn_orig(2)
+        nc.scalar.activation(out=first_table[:], in_=neg_half[:], func=ACT.Gelu)
+        copy_out(1)
+        max_of_quarters(2)
+        add_biases(0)
+        quantise_and_multiply(1)
+        mean(0)
+        on_scalar(2, range(2, 4))
+        on_vector(2, range(6, 7))
+        max_of_two(2)
+        variance(0)
+        on_scalar(2, [MAXIMUM])
+        add_biases(1)
+        centre(0, whole)
+        on_scalar(2, range(4, 5))
+        mean(1)
+        on_vector(2, range(7, 8))
+        normalise(0, whole)
+        on_scalar(2, range(5, 6))
+        variance(1)
+        copy_out_orig(2)
+        load(2 + RAG_BUFS)
+
+        for step in range(3, TILES):
+            pooling, multiplying, norming, ending = step, step - 1, step - 2, step - 3
+            gelu(ending, whole)
             max_of_halves(pooling)
-            if step == 0:
-                sum_gates(0, GATES_ON_VECTOR)
-            for k in early:
-                widen(pooling, k, True)
-                turn(pooling, k)
-            on_scalar(1)
-            if norm:
-                for g in range(HALF_PASSES):
-                    copy_out_pooled(multiplying, g)
-                centre(norming, whole)
-                normalise(norming, whole)
-            on_scalar(2)
-            if norm:
-                quantise(multiplying, 0, PASSES)
-                for n in range(N_HALVES):
-                    multiply(multiplying, n, 0, PASSES)
-            max_of_four(pooling)
-            if norm:
-                gelu(norming, whole)
-            if step == 0:
-                sum_gates(GATES_ON_VECTOR, GATES_AHEAD)
-                for t in range(GATES_AHEAD, TILES):
-                    gate(t)
-            on_scalar(1)
+            on_scalar(pooling, range(0, 1))
             turn_orig(pooling)
-            for k in late[:-1]:
-                widen(pooling, k, True)
-                turn(pooling, k)
-            if mult and not norm:
-                for g in range(HALF_PASSES):
-                    copy_out_pooled(multiplying, g)
-                quantise(multiplying, 0, PASSES)
-                for n in range(N_HALVES):
-                    multiply(multiplying, n, 0, PASSES)
-                sum_gates(GATES_AHEAD, TILES)
-            widen(pooling, MAXIMUM, False)
-            turn(pooling, MAXIMUM)
-            if mult:
-                for n in range(N_HALVES):
-                    add_bias(multiplying, n)
-            on_scalar(1)
-            widen(pooling, late[-1], True)
-            turn(pooling, late[-1])
-            if mult:
-                mean(multiplying)
-            if norm:
-                residual(norming, whole)
-            if mult:
-                variance(multiplying)
+            copy_out(multiplying)
+            residual(ending, whole)
+            quantise_and_multiply(multiplying)
+            max_of_quarters(pooling)
+            on_scalar(pooling, range(1, 3))
+            on_vector(pooling, range(6, 7))
+            max_of_two(pooling)
+            on_scalar(pooling, range(3, 4))
+            on_scalar(pooling, [MAXIMUM])
+            add_biases(multiplying)
+            centre(norming, whole)
+            on_scalar(pooling, range(4, 5))
+            mean(multiplying)
+            on_vector(pooling, range(7, 8))
+            normalise(norming, whole)
+            on_scalar(pooling, range(5, 6))
+            variance(multiplying)
             copy_out_orig(pooling)
-            on_scalar(1)
-            if live(pooling + RAG_BUFS):
-                load_refs(pooling + RAG_BUFS)
-                if (pooling + RAG_BUFS) % J == 0:
-                    load_orig((pooling + RAG_BUFS) // J)
+            load(pooling + RAG_BUFS)
+
+        ending, norming = last - 2, last - 1
+        gelu(ending, whole)
+        quantise(last, 0, HALF_PASSES)
+        for n in range(N_HALVES):
+            multiply(last, n, 0, HALF_PASSES)
+        residual(ending, whole)
+        copy_out_pooled(last, 0)
+        copy_out_pooled(last, 1, True)
+        for g in range(HALF_PASSES, PASSES):
+            quantise(last, g, g + 1)
+            for n in range(N_HALVES):
+                multiply(last, n, g, g + 1)
+        centre(norming, whole)
+        add_biases(last)
+        mean(last)
+        variance(last)
+        normalise(norming, whole)
+        gelu(norming, whole)
+        for cols in halves:
+            centre(last, cols)
+        residual(norming, whole)
+        for cols in halves:
+            normalise(last, cols)
+            gelu(last, cols)
+        for cols in halves:
+            residual(last, cols)

@@ -108,34 +108,33 @@ def tile_rarevariantawarefusion_pa_kernel(
         first_table = const.tile([P, 1], F32)
         nc.scalar.activation(out=first_table[:], in_=neg_half[:], func=ACT.Sigmoid)
 
-        cols_ps = psum.tile([P, P], BF16, tag="oT")
+        cols_ps = psum.tile([P, P], BF16, tag="oT", bufs=1)
         nc.tensor.transpose(cols_ps[:], vec_rows[:], ident_bf[:])
         vec_cols = const.tile([P, 4 * BLOCKS], BF16)
         nc.vector.tensor_copy(out=vec_cols[:], in_=cols_ps[:, 0 : 4 * BLOCKS])
         b2_cols = const.tile([P, BLOCKS], F32)
         nc.vector.tensor_copy(out=b2_cols[:], in_=cols_ps[:, 0:BLOCKS])
 
-        def turn_spread(v):
-            spread_ps = psum.tile([P, BLOCKS, P], BF16, tag="oT", name="spread_ps")
+        def turn_spread(v, tag, bufs):
+            spread_ps = psum.tile([P, D], BF16, tag=tag, bufs=bufs, name="spread_ps")
             for c in range(BLOCKS):
                 col = v * BLOCKS + c
-                nc.tensor.transpose(spread_ps[:, c, :], vec_cols[:, col : col + 1].to_broadcast([P, P]), ident_bf[:])
+                nc.tensor.transpose(
+                    spread_ps[:, c * P : (c + 1) * P], vec_cols[:, col : col + 1].to_broadcast([P, P]), ident_bf[:]
+                )
             return spread_ps
 
         def keep_spread(v, spread_ps):
             everywhere = const.tile([P, D], BF16, name="everywhere%d" % v)
-            nc.vector.tensor_copy(out=everywhere[:], in_=spread_ps[:].rearrange("p c m -> p (c m)"))
+            nc.vector.tensor_copy(out=everywhere[:], in_=spread_ps[:])
             return everywhere
 
-        def spread(v):
-            return keep_spread(v, turn_spread(v))
-
-        hT_ps = psum.tile([P, TILES, P], BF16, tag="oT")
+        hT_ps = psum.tile([P, TILES, P], BF16, tag="acc")
         for t in range(TILES):
             nc.tensor.transpose(hT_ps[:, t, :], haf[:, t // J, t % J, :], ident_bf[:])
         hT = const.tile([P, TILES, P], BF16)
         nc.scalar.copy(out=hT[:], in_=hT_ps[:])
-        b2_bc = spread(0)
+        b2_bc = keep_spread(0, turn_spread(0, "acc", 2))
         s_parts = const.tile([P, N_HALVES, TILES], F32)
         s_all = const.tile([P, TILES], F32)
 
@@ -174,11 +173,11 @@ def tile_rarevariantawarefusion_pa_kernel(
             )
             nc.vector.tensor_scalar_mul(out=s_max[:, first:last], in0=s_all[:, first:last], scalar1=MAX_W * REFS / MEAN_W)
 
+        biasf_bc = keep_spread(1, turn_spread(1, "oT", 1))
+        lng_ps = turn_spread(2, "lng", 1)
         gate(0)
-        f_ps = turn_spread(1)
-        gate(1)
-        g_ps = turn_spread(2)
-        for t in range(2, TILES):
+        b_ps = turn_spread(3, "oT", 1)
+        for t in range(1, TILES):
             gate(t)
 
         def spread_of_af():
@@ -205,29 +204,33 @@ def tile_rarevariantawarefusion_pa_kernel(
             m4 = maxima[t]
             nc.vector.tensor_tensor(out=m4[:, 0], in0=m4[:, 0], in1=m4[:, 1], op=ALU.max)
 
-        def widen(t, term, on_vector):
+        def widen(t, term, engine, first=0, last=HALF_PASSES):
             if t not in wide:
                 wide[t] = terms.tile([P, TERMS, PACK, HALF_PASSES, P], F32, name="wide")
             row = maxima[t][:, 0, :] if term == MAXIMUM else refs[t][:, term, :]
             factor = (s_max if term == MAXIMUM else s_all)[:, t : t + 1]
-            out_view = wide[t][:, term].rearrange("p i g (c j) -> p (g c) i j", j=LINE)
-            in_view = row.rearrange("p (c j i) -> p c i j", j=LINE, i=PACK)
-            if on_vector:
+            out_view = wide[t][:, term, :, first:last].rearrange("p i g (c j) -> p (g c) i j", j=LINE)
+            in_view = row[:, first * K_PASS : last * K_PASS].rearrange("p (c j i) -> p c i j", j=LINE, i=PACK)
+            if engine == "vector":
                 nc.vector.tensor_scalar_mul(out=out_view, in0=in_view, scalar1=factor)
+            elif engine == "gpsimd":
+                nc.gpsimd.tensor_scalar(
+                    out=out_view, in0=in_view, scalar1=factor, scalar2=0.0, op0=ALU.mult, op1=ALU.add
+                )
             else:
                 nc.scalar.activation(out=out_view, in_=in_view, func=ACT.Copy, scale=factor)
 
         def turn_orig(t):
             o_words = orig_sb[t // J][:, t % J, :].bitcast(F32)
-            orig_t[t] = psum.tile([P, HALF_PASSES, 2, P], F32, tag="oT", name="orig_t")
+            orig_t[t] = psum.tile([P, HALF_PASSES, 2, P], F32, tag="oT", bufs=1, name="orig_t")
             for g in range(HALF_PASSES):
                 for u in range(2):
                     nc.tensor.transpose(orig_t[t][:, g, u, :], o_words[:, 256 * g + u : 256 * (g + 1) : 2], ident_f32[:])
 
-        def turn(t, term):
-            turned[t] = turned.get(t, 0) + 1
-            for g in range(HALF_PASSES):
-                if turned[t] == 1:
+        def turn(t, term, first=0, last=HALF_PASSES):
+            for g in range(first, last):
+                turned[t, g] = turned.get((t, g), 0) + 1
+                if turned[t, g] == 1:
                     pooled_t[t, g] = psum.tile([P, PACK, P], F32, tag="pT", bufs=4, name="pooled_t")
                 for i in range(PACK):
                     nc.tensor.matmul(
@@ -235,8 +238,8 @@ def tile_rarevariantawarefusion_pa_kernel(
                         lhsT=wide[t][:, term, i, g, :],
                         rhs=ident_f32[:],
                         is_transpose=True,
-                        start=(turned[t] == 1 and i == 0),
-                        stop=(turned[t] == TERMS and i == PACK - 1),
+                        start=(turned[t, g] == 1 and i == 0),
+                        stop=(turned[t, g] == TERMS and i == PACK - 1),
                     )
 
         def copy_out_orig(t):
@@ -321,7 +324,7 @@ def tile_rarevariantawarefusion_pa_kernel(
 
         def centre(t, cols):
             nc.vector.scalar_tensor_tensor(
-                out=y[t][:, cols], in0=y[t][:, cols], scalar=neg_mean[t][:], in1=lng_bc[:, cols], op0=ALU.add, op1=ALU.mult
+                out=y[t][:, cols], in0=y[t][:, cols], scalar=neg_mean[t][:], in1=lng_ps[:, cols], op0=ALU.add, op1=ALU.mult
             )
 
         def normalise(t, cols):
@@ -351,15 +354,19 @@ def tile_rarevariantawarefusion_pa_kernel(
         halves = [slice(n * N_TILE, (n + 1) * N_TILE) for n in range(N_HALVES)]
         last = TILES - 1
 
+        def pool_terms(engine, t, terms):
+            for term in terms:
+                widen(t, term, engine)
+                turn(t, term)
+
         def on_vector(t, terms):
-            for k in terms:
-                widen(t, k, True)
-                turn(t, k)
+            pool_terms("vector", t, terms)
 
         def on_scalar(t, terms):
-            for k in terms:
-                widen(t, k, False)
-                turn(t, k)
+            pool_terms("scalar", t, terms)
+
+        def on_gpsimd(t, terms):
+            pool_terms("gpsimd", t, terms)
 
         def copy_out(t):
             for g in range(HALF_PASSES):
@@ -382,9 +389,7 @@ def tile_rarevariantawarefusion_pa_kernel(
 
         max_of_halves(0)
         sum_gates(0, 1)
-        biasf_bc = keep_spread(1, f_ps)
-        lng_bc = keep_spread(2, g_ps)
-        b_ps = turn_spread(3)
+        lnb_bc = keep_spread(3, b_ps)
         turn_orig(0)
         on_vector(0, range(0, 3))
         max_of_quarters(0)
@@ -395,7 +400,6 @@ def tile_rarevariantawarefusion_pa_kernel(
         on_scalar(0, [MAXIMUM])
         on_scalar(0, range(6, 8))
         sum_gates(1, TILES)
-        lnb_bc = keep_spread(3, b_ps)
         af_scale = spread_of_af()
         load(RAG_BUFS)
 
@@ -434,34 +438,33 @@ def tile_rarevariantawarefusion_pa_kernel(
         on_vector(2, range(7, 8))
         normalise(0, whole)
         on_scalar(2, range(5, 6))
-        variance(1)
         copy_out_orig(2)
         load(2 + RAG_BUFS)
 
         for step in range(3, TILES):
             pooling, multiplying, norming, ending = step, step - 1, step - 2, step - 3
-            gelu(ending, whole)
             max_of_halves(pooling)
             on_scalar(pooling, range(0, 1))
             turn_orig(pooling)
             copy_out(multiplying)
-            residual(ending, whole)
+            gelu(ending, whole)
+            variance(norming)
             quantise_and_multiply(multiplying)
             max_of_quarters(pooling)
+            residual(ending, whole)
             on_scalar(pooling, range(1, 3))
-            on_vector(pooling, range(6, 7))
+            on_vector(pooling, [6])
             max_of_two(pooling)
             on_scalar(pooling, range(3, 4))
-            on_scalar(pooling, [MAXIMUM])
             add_biases(multiplying)
+            on_gpsimd(pooling, [MAXIMUM])
             centre(norming, whole)
             on_scalar(pooling, range(4, 5))
-            mean(multiplying)
-            on_vector(pooling, range(7, 8))
-            normalise(norming, whole)
-            on_scalar(pooling, range(5, 6))
-            variance(multiplying)
+            on_gpsimd(pooling, [7])
             copy_out_orig(pooling)
+            normalise(norming, whole)
+            mean(multiplying)
+            on_scalar(pooling, range(5, 6))
             load(pooling + RAG_BUFS)
 
         ending, norming = last - 2, last - 1
@@ -471,6 +474,7 @@ def tile_rarevariantawarefusion_pa_kernel(
             multiply(last, n, 0, HALF_PASSES)
         residual(ending, whole)
         copy_out_pooled(last, 0)
+        variance(norming)
         copy_out_pooled(last, 1, True)
         for g in range(HALF_PASSES, PASSES):
             quantise(last, g, g + 1)

@@ -29,7 +29,7 @@ MEAN_W, MAX_W = 0.7, 0.3
 MAXIMUM = REFS
 TERMS = REFS + 1
 LINE = 4
-GATES_BY_TRANSPOSES = 2
+GATES_ON_VECTOR = (0, 1)
 RAG_BUFS = 4
 
 FLOPS = 2 * B * L * (2 * D) * D + 2 * B * L * H * D
@@ -49,7 +49,7 @@ def tile_rarevariantawarefusion_pa_kernel(
         ctx.enter_context(tc.manual_schedule())
 
         orig_sb, refs, maxima, wide, turned, orig_t, pooled_t, grouped = {}, {}, {}, {}, {}, {}, {}, {}
-        x_codes, x_planes, acc, y, y_sum, neg_mean, rstd, res = {}, {}, {}, {}, {}, {}, {}, {}
+        x_codes, x_planes, acc, y, y_sum, neg_mean, sq_sum, var_eps, rstd, yn, res = {}, {}, {}, {}, {}, {}, {}, {}, {}, {}, {}
 
         def live(t):
             return 0 <= t < TILES
@@ -68,16 +68,16 @@ def tile_rarevariantawarefusion_pa_kernel(
                 nc.sync.dma_start(out=r_t[:, k : k + REFS // 2], in_=rows[:, k : k + REFS // 2])
             refs[t] = r_t
 
+        vec_rows = const.tile([P, P], BF16)
+        nc.vector.memset(vec_rows[:], 0.0)
+        for v, vec in enumerate((b2, ln_g)):
+            nc.sync.dma_start(out=vec_rows[v * BLOCKS : (v + 1) * BLOCKS, :], in_=vec.rearrange("(c m) -> c m", m=P))
         haf = const.tile([P, B, J, H], BF16)
         nc.sync.dma_start(
             out=haf[:].rearrange("p b j h -> p b (j h)"), in_=h_af.rearrange("b (p j) h -> p b (j h)", j=J)
         )
         w2_sb = const.tile([P, D], BF16)
         nc.sync.dma_start(out=w2_sb[:], in_=w2)
-        vec_rows = const.tile([P, P], BF16)
-        nc.vector.memset(vec_rows[:], 0.0)
-        for v, vec in enumerate((b2, bias_f, ln_g, ln_b)):
-            nc.sync.dma_start(out=vec_rows[v * BLOCKS : (v + 1) * BLOCKS, :], in_=vec.rearrange("(c m) -> c m", m=P))
         af_sb = const.tile([P, B, J], BF16)
         nc.sync.dma_start(out=af_sb[:], in_=af.rearrange("b (p j) -> p b j", j=J))
         load_refs(0)
@@ -92,6 +92,10 @@ def tile_rarevariantawarefusion_pa_kernel(
         nc.sync.dma_start(out=w_words[:].bitcast(I32), in_=wf_words.rearrange("g p n -> p g n").bitcast(I32))
         load_refs(2)
         load_orig(1)
+        biasf_bc = const.tile([P, D], BF16)
+        nc.sync.dma_start(out=biasf_bc[:], in_=bias_f.partition_broadcast(P))
+        lnb_bc = const.tile([P, D], BF16)
+        nc.sync.dma_start(out=lnb_bc[:], in_=ln_b.partition_broadcast(P))
         load_refs(3)
 
         ident_bf = const.tile([P, P], BF16)
@@ -110,10 +114,8 @@ def tile_rarevariantawarefusion_pa_kernel(
 
         cols_ps = psum.tile([P, P], BF16, tag="oT", bufs=1)
         nc.tensor.transpose(cols_ps[:], vec_rows[:], ident_bf[:])
-        vec_cols = const.tile([P, 4 * BLOCKS], BF16)
-        nc.vector.tensor_copy(out=vec_cols[:], in_=cols_ps[:, 0 : 4 * BLOCKS])
-        b2_cols = const.tile([P, BLOCKS], F32)
-        nc.vector.tensor_copy(out=b2_cols[:], in_=cols_ps[:, 0:BLOCKS])
+        vec_cols = const.tile([P, 2 * BLOCKS], BF16)
+        nc.vector.tensor_copy(out=vec_cols[:], in_=cols_ps[:, 0 : 2 * BLOCKS])
 
         def turn_spread(v, tag, bufs):
             spread_ps = psum.tile([P, D], BF16, tag=tag, bufs=bufs, name="spread_ps")
@@ -124,45 +126,35 @@ def tile_rarevariantawarefusion_pa_kernel(
                 )
             return spread_ps
 
-        def keep_spread(v, spread_ps):
-            everywhere = const.tile([P, D], BF16, name="everywhere%d" % v)
-            nc.vector.tensor_copy(out=everywhere[:], in_=spread_ps[:])
-            return everywhere
-
         hT_ps = psum.tile([P, TILES, P], BF16, tag="acc")
         for t in range(TILES):
             nc.tensor.transpose(hT_ps[:, t, :], haf[:, t // J, t % J, :], ident_bf[:])
         hT = const.tile([P, TILES, P], BF16)
         nc.scalar.copy(out=hT[:], in_=hT_ps[:])
-        b2_bc = keep_spread(0, turn_spread(0, "acc", 2))
+        b2_ps = turn_spread(0, "acc", 2)
+        b2_bc = const.tile([P, D], BF16)
+        nc.vector.tensor_copy(out=b2_bc[:], in_=b2_ps[:])
         s_parts = const.tile([P, N_HALVES, TILES], F32)
         s_all = const.tile([P, TILES], F32)
 
         def gate(t):
+            on_vector = t in GATES_ON_VECTOR
             for n in range(N_HALVES):
-                if t % 3 < 2:
+                if t % 3 < 2 and t < TILES - 1:
                     z_ps = psum.tile([P, N_TILE], F32, tag="pT", bufs=4)
                 else:
                     z_ps = psum.tile([P, N_TILE], F32, tag="acc")
                 cols = slice(n * N_TILE, (n + 1) * N_TILE)
-                nc.tensor.matmul(z_ps[:], lhsT=hT[:, t, :], rhs=w2_sb[:, cols], start=True, stop=False)
-                if t < GATES_BY_TRANSPOSES:
-                    chunks = N_TILE // P
-                    for c in range(chunks):
-                        col = n * chunks + c
-                        nc.tensor.matmul(
-                            z_ps[:, c * P : (c + 1) * P],
-                            lhsT=b2_cols[:, col : col + 1].to_broadcast([P, P]),
-                            rhs=ident_f32[:],
-                            is_transpose=True,
-                            start=False,
-                            stop=(c == chunks - 1),
-                        )
+                nc.tensor.matmul(z_ps[:], lhsT=hT[:, t, :], rhs=w2_sb[:, cols], start=True, stop=on_vector)
+                if on_vector:
+                    logits = work.tile([P, N_TILE], F32, tag="yn", bufs=3, name="logits")
+                    nc.vector.tensor_tensor(out=logits[:], in0=z_ps[:], in1=b2_bc[:, cols], op=ALU.add)
                 else:
                     nc.tensor.matmul(z_ps[:], lhsT=first_row[:], rhs=b2_bc[:, cols], start=False, stop=True)
-                gates = work.tile([P, N_TILE], BF16, name="gates")
+                    logits = z_ps
+                gates = work.tile([P, N_TILE], BF16, tag="unread", name="gates")
                 nc.scalar.activation(
-                    out=gates[:], in_=z_ps[:], func=ACT.Sigmoid, accum_out=s_parts[:, n, t : t + 1]
+                    out=gates[:], in_=logits[:], func=ACT.Sigmoid, accum_out=s_parts[:, n, t : t + 1]
                 )
 
         s_max = const.tile([P, TILES], F32)
@@ -173,12 +165,10 @@ def tile_rarevariantawarefusion_pa_kernel(
             )
             nc.vector.tensor_scalar_mul(out=s_max[:, first:last], in0=s_all[:, first:last], scalar1=MAX_W * REFS / MEAN_W)
 
-        biasf_bc = keep_spread(1, turn_spread(1, "oT", 1))
-        lng_ps = turn_spread(2, "lng", 1)
-        gate(0)
-        b_ps = turn_spread(3, "oT", 1)
-        for t in range(1, TILES):
+        for t in range(TILES - 2):
             gate(t)
+        lng_ps = turn_spread(1, "lng", 1)
+        gate(TILES - 2)
 
         def spread_of_af():
             af_flat = af_sb[:].rearrange("p b j -> p (b j)")
@@ -311,36 +301,49 @@ def tile_rarevariantawarefusion_pa_kernel(
                 op1=ALU.mult,
             )
 
-        def variance(t):
+        def square(t):
             squares = work.tile([P, D], BF16, tag="unread")
-            sq_sum = work.tile([P, 1], F32)
-            nc.scalar.activation(out=squares[:], in_=y[t][:], func=ACT.Square, bias=neg_mean[t][:], accum_out=sq_sum[:])
-            var_eps = work.tile([P, 1], F32)
-            nc.gpsimd.tensor_scalar(
-                out=var_eps[:], in0=sq_sum[:], scalar1=1.0 / D, scalar2=LN_EPS, op0=ALU.mult, op1=ALU.add
+            sq_sum[t] = work.tile([P, 1], F32, name="sq_sum")
+            nc.scalar.activation(
+                out=squares[:], in_=y[t][:], func=ACT.Square, bias=neg_mean[t][:], accum_out=sq_sum[t][:]
             )
+
+        def add_eps(t, engine):
+            var_eps[t] = work.tile([P, 1], F32, name="var_eps")
+            engine.tensor_scalar(
+                out=var_eps[t][:], in0=sq_sum[t][:], scalar1=1.0 / D, scalar2=LN_EPS, op0=ALU.mult, op1=ALU.add
+            )
+
+        def invert_root(t):
             rstd[t] = work.tile([P, 1], F32, name="rstd")
-            nc.gpsimd.tensor_tensor(out=rstd[t][:], in0=var_eps[:], in1=neg_half[:], op=ALU.pow)
+            nc.gpsimd.tensor_tensor(out=rstd[t][:], in0=var_eps[t][:], in1=neg_half[:], op=ALU.pow)
+
+        def variance(t):
+            square(t)
+            add_eps(t, nc.gpsimd)
+            invert_root(t)
 
         def centre(t, cols):
+            if cols.start == 0:
+                yn[t] = work.tile([P, D], F32, tag="yn", bufs=3, name="yn")
             nc.vector.scalar_tensor_tensor(
-                out=y[t][:, cols], in0=y[t][:, cols], scalar=neg_mean[t][:], in1=lng_ps[:, cols], op0=ALU.add, op1=ALU.mult
+                out=yn[t][:, cols], in0=y[t][:, cols], scalar=neg_mean[t][:], in1=lng_ps[:, cols], op0=ALU.add, op1=ALU.mult
             )
 
         def normalise(t, cols):
             nc.vector.scalar_tensor_tensor(
-                out=y[t][:, cols], in0=y[t][:, cols], scalar=rstd[t][:], in1=lnb_bc[:, cols], op0=ALU.mult, op1=ALU.add
+                out=yn[t][:, cols], in0=yn[t][:, cols], scalar=rstd[t][:], in1=lnb_bc[:, cols], op0=ALU.mult, op1=ALU.add
             )
 
         def gelu(t, cols):
-            nc.scalar.activation(out=y[t][:, cols], in_=y[t][:, cols], func=ACT.Gelu)
+            nc.scalar.activation(out=yn[t][:, cols], in_=yn[t][:, cols], func=ACT.Gelu)
 
         def residual(t, cols):
             if cols.start == 0:
                 res[t] = work.tile([P, D], F32, name="res")
             nc.vector.scalar_tensor_tensor(
                 out=res[t][:, cols],
-                in0=y[t][:, cols],
+                in0=yn[t][:, cols],
                 scalar=af_scale[:, t : t + 1],
                 in1=orig_sb[t // J][:, t % J, cols],
                 op0=ALU.mult,
@@ -389,36 +392,36 @@ def tile_rarevariantawarefusion_pa_kernel(
 
         max_of_halves(0)
         sum_gates(0, 1)
-        lnb_bc = keep_spread(3, b_ps)
-        turn_orig(0)
-        on_vector(0, range(0, 3))
+        on_vector(0, [0, 1])
+        gate(TILES - 1)
+        on_vector(0, [2])
         max_of_quarters(0)
-        on_vector(0, range(3, 4))
+        turn_orig(0)
+        on_vector(0, [3])
         max_of_two(0)
-        on_vector(0, range(4, 6))
+        on_vector(0, [4, 5])
         copy_out_orig(0)
-        on_scalar(0, [MAXIMUM])
-        on_scalar(0, range(6, 8))
+        on_scalar(0, [MAXIMUM, 6, 7])
         sum_gates(1, TILES)
         af_scale = spread_of_af()
         load(RAG_BUFS)
 
         max_of_halves(1)
         turn_orig(1)
-        on_scalar(1, range(0, 3))
+        on_scalar(1, [0, 1])
         max_of_quarters(1)
-        on_vector(1, range(5, 6))
+        on_vector(1, [4])
         max_of_two(1)
-        on_vector(1, range(6, 8))
-        on_scalar(1, [MAXIMUM])
         copy_out(0)
+        on_vector(1, [5, 6, 7])
+        on_scalar(1, [MAXIMUM])
         copy_out_orig(1)
         quantise_and_multiply(0)
-        on_scalar(1, range(3, 5))
+        on_scalar(1, [2, 3])
         load(1 + RAG_BUFS)
 
         max_of_halves(2)
-        on_scalar(2, range(0, 2))
+        on_scalar(2, [0, 1])
         turn_orig(2)
         nc.scalar.activation(out=first_table[:], in_=neg_half[:], func=ACT.Gelu)
         copy_out(1)
@@ -426,25 +429,27 @@ def tile_rarevariantawarefusion_pa_kernel(
         add_biases(0)
         quantise_and_multiply(1)
         mean(0)
-        on_scalar(2, range(2, 4))
-        on_vector(2, range(6, 7))
+        on_scalar(2, [2])
+        on_scalar(2, [3])
+        on_vector(2, [6])
+        on_vector(2, [7])
         max_of_two(2)
         variance(0)
         on_scalar(2, [MAXIMUM])
         add_biases(1)
         centre(0, whole)
-        on_scalar(2, range(4, 5))
-        mean(1)
-        on_vector(2, range(7, 8))
-        normalise(0, whole)
-        on_scalar(2, range(5, 6))
+        on_scalar(2, [4])
         copy_out_orig(2)
+        mean(1)
+        normalise(0, whole)
+        on_scalar(2, [5])
         load(2 + RAG_BUFS)
 
         for step in range(3, TILES):
             pooling, multiplying, norming, ending = step, step - 1, step - 2, step - 3
             max_of_halves(pooling)
-            on_scalar(pooling, range(0, 1))
+            on_scalar(pooling, [0])
+            on_vector(pooling, [6])
             turn_orig(pooling)
             copy_out(multiplying)
             gelu(ending, whole)
@@ -452,45 +457,47 @@ def tile_rarevariantawarefusion_pa_kernel(
             quantise_and_multiply(multiplying)
             max_of_quarters(pooling)
             residual(ending, whole)
-            on_scalar(pooling, range(1, 3))
-            on_vector(pooling, [6])
+            on_scalar(pooling, [1])
+            on_scalar(pooling, [2])
             max_of_two(pooling)
-            on_scalar(pooling, range(3, 4))
+            on_scalar(pooling, [3])
             add_biases(multiplying)
             on_gpsimd(pooling, [MAXIMUM])
             centre(norming, whole)
-            on_scalar(pooling, range(4, 5))
+            on_scalar(pooling, [4])
             on_gpsimd(pooling, [7])
             copy_out_orig(pooling)
             normalise(norming, whole)
             mean(multiplying)
-            on_scalar(pooling, range(5, 6))
+            on_scalar(pooling, [5])
             load(pooling + RAG_BUFS)
 
         ending, norming = last - 2, last - 1
-        gelu(ending, whole)
         quantise(last, 0, HALF_PASSES)
         for n in range(N_HALVES):
             multiply(last, n, 0, HALF_PASSES)
-        residual(ending, whole)
+        gelu(ending, whole)
+        centre(norming, whole)
         copy_out_pooled(last, 0)
-        variance(norming)
         copy_out_pooled(last, 1, True)
         for g in range(HALF_PASSES, PASSES):
             quantise(last, g, g + 1)
             for n in range(N_HALVES):
                 multiply(last, n, g, g + 1)
-        centre(norming, whole)
+        variance(norming)
+        residual(ending, whole)
         add_biases(last)
         mean(last)
-        variance(last)
+        square(last)
+        for cols in halves:
+            centre(last, cols)
+        add_eps(last, nc.vector)
+        invert_root(last)
         normalise(norming, whole)
         gelu(norming, whole)
         for cols in halves:
-            centre(last, cols)
-        residual(norming, whole)
-        for cols in halves:
             normalise(last, cols)
             gelu(last, cols)
+        residual(norming, whole)
         for cols in halves:
             residual(last, cols)

from contextlib import ExitStack

import concourse.mybir as mybir
from concourse.masks import make_identity

F32 = mybir.dt.float32
BF16 = mybir.dt.bfloat16
I32 = mybir.dt.int32
U32 = mybir.dt.uint32
U8 = mybir.dt.uint8
FP8X4 = mybir.dt.float8_e4m3fn_x4
FP4X4 = mybir.dt.float4_e2m1fn_x4
ALU = mybir.AluOpType
ACT = mybir.ActivationFunctionType

P = 128
B, REFS, L, D, H = 4, 8, 256, 1024, 128
J = L // P
TILES = B * J
BLOCKS = D // P
PACK = 4
K_PASS = P * PACK
PASSES = 2 * D // K_PASS
HALF_PASSES = PASSES // 2
N_TILE = 512
N_HALVES = D // N_TILE
LN_EPS = 1e-5
MEAN_W, MAX_W = 0.7, 0.3
MAXIMUM = REFS
TERMS = REFS + 1
LINE = 4
GATES_ON_VECTOR = (0, 1)
RAG_BUFS = 4

FLOPS = 2 * B * L * (2 * D) * D + 2 * B * L * H * D


def tile_rarevariantawarefusion_pa_kernel(
    tc, orig_feat, rag_feat, af, h_af, w2, b2, wf_words, wf_scales, bias_f, ln_g, ln_b, out
):
    nc = tc.nc
    with ExitStack() as ctx:
        const = ctx.enter_context(tc.tile_pool(name="const", bufs=1))
        origs = ctx.enter_context(tc.tile_pool(name="origs", bufs=B))
        rags = ctx.enter_context(tc.tile_pool(name="rags", bufs=RAG_BUFS))
        terms = ctx.enter_context(tc.tile_pool(name="terms", bufs=2))
        work = ctx.enter_context(tc.tile_pool(name="work", bufs=2))
        psum = ctx.enter_context(tc.psum_pool(name="psum", bufs=2))
        ctx.enter_context(tc.manual_schedule())

        orig_sb, refs, maxima, wide, turned, orig_t, pooled_t, grouped = {}, {}, {}, {}, {}, {}, {}, {}
        x_codes, x_planes, acc, y, y_sum, neg_mean, sq_sum, var_eps, rstd, yn, res = {}, {}, {}, {}, {}, {}, {}, {}, {}, {}, {}

        def live(t):
            return 0 <= t < TILES

        def load_orig(b):
            o_t = origs.tile([P, J, D], BF16, name="o_t")
            nc.sync.dma_start(
                out=o_t[:].rearrange("p j d -> p (j d)"), in_=orig_feat[b].rearrange("(p j) d -> p (j d)", j=J)
            )
            orig_sb[b] = o_t

        def load_refs(t):
            r_t = rags.tile([P, REFS, D], BF16, name="r_t")
            rows = rag_feat[t // J].rearrange("k (p j) d -> j p k d", j=J)[t % J]
            for k in range(0, REFS, REFS // 2):
                nc.sync.dma_start(out=r_t[:, k : k + REFS // 2], in_=rows[:, k : k + REFS // 2])
            refs[t] = r_t

        vec_rows = const.tile([P, P], BF16)
        nc.vector.memset(vec_rows[:], 0.0)
        for v, vec in enumerate((b2, ln_g)):
            nc.sync.dma_start(out=vec_rows[v * BLOCKS : (v + 1) * BLOCKS, :], in_=vec.rearrange("(c m) -> c m", m=P))
        haf = const.tile([P, B, J, H], BF16)
        nc.sync.dma_start(
            out=haf[:].rearrange("p b j h -> p b (j h)"), in_=h_af.rearrange("b (p j) h -> p b (j h)", j=J)
        )
        w2_sb = const.tile([P, D], BF16)
        nc.sync.dma_start(out=w2_sb[:], in_=w2)
        af_sb = const.tile([P, B, J], BF16)
        nc.sync.dma_start(out=af_sb[:], in_=af.rearrange("b (p j) -> p b j", j=J))
        load_refs(0)
        load_orig(0)
        load_refs(1)
        w_planes = const.tile([P, PASSES, D], U8, align_bytes=64)
        nc.vector.memset(w_planes[:].bitcast(I32), 0)
        scale_rows = wf_scales.bitcast(I32).rearrange("g (q r) n -> r q g n", r=4)
        for r in range(4):
            nc.sync.dma_start(out=w_planes[:].bitcast(I32)[r:P:32], in_=scale_rows[r])
        w_words = const.tile([P, PASSES, 2 * D], U8, align_bytes=64)
        nc.sync.dma_start(out=w_words[:].bitcast(I32), in_=wf_words.rearrange("g p n -> p g n").bitcast(I32))
        load_refs(2)
        load_orig(1)
        biasf_bc = const.tile([P, D], BF16)
        nc.sync.dma_start(out=biasf_bc[:], in_=bias_f.partition_broadcast(P))
        lnb_bc = const.tile([P, D], BF16)
        nc.sync.dma_start(out=lnb_bc[:], in_=ln_b.partition_broadcast(P))
        load_refs(3)

        ident_bf = const.tile([P, P], BF16)
        make_identity(nc, ident_bf[:])
        ident_f32 = const.tile([P, P], F32)
        make_identity(nc, ident_f32[:])
        half = const.tile([P, TILES], F32)
        nc.vector.memset(half[:], 0.5)
        neg_half = const.tile([P, 1], F32)
        nc.vector.memset(neg_half[:], -0.5)
        first_row = const.tile([P, P], BF16)
        nc.vector.memset(first_row[:], 0.0)
        nc.vector.memset(first_row[0:1, :], 1.0)
        first_table = const.tile([P, 1], F32)
        nc.scalar.activation(out=first_table[:], in_=neg_half[:], func=ACT.Sigmoid)

        cols_ps = psum.tile([P, P], BF16, tag="oT", bufs=1)
        nc.tensor.transpose(cols_ps[:], vec_rows[:], ident_bf[:])
        vec_cols = const.tile([P, 2 * BLOCKS], BF16)
        nc.vector.tensor_copy(out=vec_cols[:], in_=cols_ps[:, 0 : 2 * BLOCKS])

        def turn_spread(v, tag, bufs):
            spread_ps = psum.tile([P, D], BF16, tag=tag, bufs=bufs, name="spread_ps")
            for c in range(BLOCKS):
                col = v * BLOCKS + c
                nc.tensor.transpose(
                    spread_ps[:, c * P : (c + 1) * P], vec_cols[:, col : col + 1].to_broadcast([P, P]), ident_bf[:]
                )
            return spread_ps

        hT_ps = psum.tile([P, TILES, P], BF16, tag="acc")
        for t in range(TILES):
            nc.tensor.transpose(hT_ps[:, t, :], haf[:, t // J, t % J, :], ident_bf[:])
        hT = const.tile([P, TILES, P], BF16)
        nc.scalar.copy(out=hT[:], in_=hT_ps[:])
        b2_ps = turn_spread(0, "acc", 2)
        b2_bc = const.tile([P, D], BF16)
        nc.vector.tensor_copy(out=b2_bc[:], in_=b2_ps[:])
        s_parts = const.tile([P, N_HALVES, TILES], F32)
        s_all = const.tile([P, TILES], F32)

        def gate(t):
            on_vector = t in GATES_ON_VECTOR
            for n in range(N_HALVES):
                if t % 3 < 2 and t < TILES - 1:
                    z_ps = psum.tile([P, N_TILE], F32, tag="pT", bufs=4)
                else:
                    z_ps = psum.tile([P, N_TILE], F32, tag="acc")
                cols = slice(n * N_TILE, (n + 1) * N_TILE)
                nc.tensor.matmul(z_ps[:], lhsT=hT[:, t, :], rhs=w2_sb[:, cols], start=True, stop=on_vector)
                if on_vector:
                    logits = work.tile([P, N_TILE], F32, tag="yn", bufs=3, name="logits")
                    nc.vector.tensor_tensor(out=logits[:], in0=z_ps[:], in1=b2_bc[:, cols], op=ALU.add)
                else:
                    nc.tensor.matmul(z_ps[:], lhsT=first_row[:], rhs=b2_bc[:, cols], start=False, stop=True)
                    logits = z_ps
                gates = work.tile([P, N_TILE], BF16, tag="unread", name="gates")
                nc.scalar.activation(
                    out=gates[:], in_=logits[:], func=ACT.Sigmoid, accum_out=s_parts[:, n, t : t + 1]
                )

        s_max = const.tile([P, TILES], F32)

        def sum_gates(first, last):
            nc.vector.tensor_tensor(
                out=s_all[:, first:last], in0=s_parts[:, 0, first:last], in1=s_parts[:, 1, first:last], op=ALU.add
            )
            nc.vector.tensor_scalar_mul(out=s_max[:, first:last], in0=s_all[:, first:last], scalar1=MAX_W * REFS / MEAN_W)

        for t in range(TILES - 2):
            gate(t)
        lng_ps = turn_spread(1, "lng", 1)
        gate(TILES - 2)

        def spread_of_af():
            af_flat = af_sb[:].rearrange("p b j -> p (b j)")
            one_minus = const.tile([P, TILES], F32)
            nc.vector.tensor_scalar(
                out=one_minus[:], in0=af_flat, scalar1=-1.0, scalar2=1.0, op0=ALU.mult, op1=ALU.add
            )
            product = const.tile([P, TILES], F32)
            nc.vector.tensor_tensor(out=product[:], in0=one_minus[:], in1=af_flat, op=ALU.mult)
            root = const.tile([P, TILES], F32)
            nc.gpsimd.tensor_tensor(out=root[:], in0=product[:], in1=half[:], op=ALU.pow)
            return root

        def max_of_halves(t):
            maxima[t] = work.tile([P, 4, D], BF16, name="maxima")
            nc.vector.tensor_tensor(out=maxima[t][:], in0=refs[t][:, 0:4], in1=refs[t][:, 4:8], op=ALU.max)

        def max_of_quarters(t):
            m4 = maxima[t]
            nc.vector.tensor_tensor(out=m4[:, 0:2], in0=m4[:, 0:2], in1=m4[:, 2:4], op=ALU.max)

        def max_of_two(t):
            m4 = maxima[t]
            nc.vector.tensor_tensor(out=m4[:, 0], in0=m4[:, 0], in1=m4[:, 1], op=ALU.max)

        def widen(t, term, engine, first=0, last=HALF_PASSES):
            if t not in wide:
                wide[t] = terms.tile([P, TERMS, PACK, HALF_PASSES, P], F32, name="wide")
            row = maxima[t][:, 0, :] if term == MAXIMUM else refs[t][:, term, :]
            factor = (s_max if term == MAXIMUM else s_all)[:, t : t + 1]
            out_view = wide[t][:, term, :, first:last].rearrange("p i g (c j) -> p (g c) i j", j=LINE)
            in_view = row[:, first * K_PASS : last * K_PASS].rearrange("p (c j i) -> p c i j", j=LINE, i=PACK)
            if engine == "vector":
                nc.vector.tensor_scalar_mul(out=out_view, in0=in_view, scalar1=factor)
            elif engine == "gpsimd":
                nc.gpsimd.tensor_scalar(
                    out=out_view, in0=in_view, scalar1=factor, scalar2=0.0, op0=ALU.mult, op1=ALU.add
                )
            else:
                nc.scalar.activation(out=out_view, in_=in_view, func=ACT.Copy, scale=factor)

        def turn_orig(t):
            o_words = orig_sb[t // J][:, t % J, :].bitcast(F32)
            orig_t[t] = psum.tile([P, HALF_PASSES, 2, P], F32, tag="oT", bufs=1, name="orig_t")
            for g in range(HALF_PASSES):
                for u in range(2):
                    nc.tensor.transpose(orig_t[t][:, g, u, :], o_words[:, 256 * g + u : 256 * (g + 1) : 2], ident_f32[:])

        def turn(t, term, first=0, last=HALF_PASSES):
            for g in range(first, last):
                turned[t, g] = turned.get((t, g), 0) + 1
                if turned[t, g] == 1:
                    pooled_t[t, g] = psum.tile([P, PACK, P], F32, tag="pT", bufs=4, name="pooled_t")
                for i in range(PACK):
                    nc.tensor.matmul(
                        pooled_t[t, g][:, i, :],
                        lhsT=wide[t][:, term, i, g, :],
                        rhs=ident_f32[:],
                        is_transpose=True,
                        start=(turned[t, g] == 1 and i == 0),
                        stop=(turned[t, g] == TERMS and i == PACK - 1),
                    )

        def copy_out_orig(t):
            grouped[t] = work.tile([P, PASSES, P, PACK], BF16, align_bytes=64, name="grouped")
            o_grouped = (
                grouped[t][:, 0:HALF_PASSES]
                .rearrange("p g r i -> p (g r i)")
                .bitcast(F32)
                .rearrange("p (g r u) -> p g r u", g=HALF_PASSES, u=2)
            )
            nc.vector.tensor_copy(out=o_grouped, in_=orig_t[t][:].rearrange("p g u r -> p g r u"))

        def copy_out_pooled(t, g, on_vector=False):
            out_view = grouped[t][:, HALF_PASSES + g]
            in_view = pooled_t[t, g][:].rearrange("p i r -> p r i")
            if on_vector:
                nc.vector.tensor_scalar_mul(out=out_view, in0=in_view, scalar1=MEAN_W / REFS)
            else:
                nc.scalar.activation(out=out_view, in_=in_view, func=ACT.Copy, scale=MEAN_W / REFS)

        def quantise(t, first, last):
            if first == 0:
                x_codes[t] = work.tile([P, PASSES * P], U32, align_bytes=64, name="x_codes")
                x_planes[t] = work.tile([P, PASSES * P], U8, align_bytes=64, name="x_planes")
            words = slice(first * P, last * P)
            nc.vector.quantize_mx(
                out=x_codes[t][:, words].bitcast(FP8X4),
                scales=x_planes[t][:, words],
                in_=grouped[t][:, first:last].rearrange("p g r i -> p (g r i)"),
            )

        def multiply(t, n, first, last):
            if first == 0:
                acc[t, n] = psum.tile([P, N_TILE], F32, tag="acc", name="acc")
            for g in range(first, last):
                nc.tensor.matmul_mx(
                    out=acc[t, n][:],
                    lhsT=x_codes[t][:, g * P : (g + 1) * P].bitcast(FP8X4),
                    lhsT_scale=x_planes[t][:, g * P : (g + 1) * P],
                    rhs=w_words[:, g, 2 * n * N_TILE : 2 * (n + 1) * N_TILE].bitcast(FP4X4),
                    rhs_scale=w_planes[:, g, n * N_TILE : (n + 1) * N_TILE],
                    start=(g == 0),
                    stop=(g == PASSES - 1),
                )

        def add_bias(t, n):
            if n == 0:
                y[t] = work.tile([P, D], F32, tag="y", name="y")
                y_sum[t] = work.tile([P, N_HALVES], F32, name="y_sum")
            cols = slice(n * N_TILE, (n + 1) * N_TILE)
            nc.vector.scalar_tensor_tensor(
                out=y[t][:, cols],
                in0=acc[t, n][:],
                scalar=1.0,
                in1=biasf_bc[:, cols],
                op0=ALU.mult,
                op1=ALU.add,
                accum_out=y_sum[t][:, n : n + 1],
            )

        def mean(t):
            neg_mean[t] = work.tile([P, 1], F32, name="neg_mean")
            nc.vector.tensor_scalar(
                out=neg_mean[t][:],
                in0=y_sum[t][:, 0:1],
                scalar1=y_sum[t][:, 1:2],
                scalar2=-1.0 / D,
                op0=ALU.add,
                op1=ALU.mult,
            )

        def square(t):
            squares = work.tile([P, D], BF16, tag="unread")
            sq_sum[t] = work.tile([P, 1], F32, name="sq_sum")
            nc.scalar.activation(
                out=squares[:], in_=y[t][:], func=ACT.Square, bias=neg_mean[t][:], accum_out=sq_sum[t][:]
            )

        def add_eps(t, engine):
            var_eps[t] = work.tile([P, 1], F32, name="var_eps")
            engine.tensor_scalar(
                out=var_eps[t][:], in0=sq_sum[t][:], scalar1=1.0 / D, scalar2=LN_EPS, op0=ALU.mult, op1=ALU.add
            )

        def invert_root(t):
            rstd[t] = work.tile([P, 1], F32, name="rstd")
            nc.gpsimd.tensor_tensor(out=rstd[t][:], in0=var_eps[t][:], in1=neg_half[:], op=ALU.pow)

        def variance(t):
            square(t)
            add_eps(t, nc.gpsimd)
            invert_root(t)

        def centre(t, cols):
            if cols.start == 0:
                yn[t] = work.tile([P, D], F32, tag="yn", bufs=3, name="yn")
            nc.vector.scalar_tensor_tensor(
                out=yn[t][:, cols], in0=y[t][:, cols], scalar=neg_mean[t][:], in1=lng_ps[:, cols], op0=ALU.add, op1=ALU.mult
            )

        def normalise(t, cols):
            nc.vector.scalar_tensor_tensor(
                out=yn[t][:, cols], in0=yn[t][:, cols], scalar=rstd[t][:], in1=lnb_bc[:, cols], op0=ALU.mult, op1=ALU.add
            )

        def gelu(t, cols):
            nc.scalar.activation(out=yn[t][:, cols], in_=yn[t][:, cols], func=ACT.Gelu)

        def residual(t, cols):
            if cols.start == 0:
                res[t] = work.tile([P, D], F32, name="res")
            nc.vector.scalar_tensor_tensor(
                out=res[t][:, cols],
                in0=yn[t][:, cols],
                scalar=af_scale[:, t : t + 1],
                in1=orig_sb[t // J][:, t % J, cols],
                op0=ALU.mult,
                op1=ALU.add,
            )
            nc.sync.dma_start(
                out=out[t // J].rearrange("(p j) d -> p j d", j=J)[:, t % J, cols], in_=res[t][:, cols]
            )

        whole = slice(0, D)
        halves = [slice(n * N_TILE, (n + 1) * N_TILE) for n in range(N_HALVES)]
        last = TILES - 1

        def pool_terms(engine, t, terms):
            for term in terms:
                widen(t, term, engine)
                turn(t, term)

        def on_vector(t, terms):
            pool_terms("vector", t, terms)

        def on_scalar(t, terms):
            pool_terms("scalar", t, terms)

        def on_gpsimd(t, terms):
            pool_terms("gpsimd", t, terms)

        def copy_out(t):
            for g in range(HALF_PASSES):
                copy_out_pooled(t, g)

        def quantise_and_multiply(t):
            quantise(t, 0, PASSES)
            for n in range(N_HALVES):
                multiply(t, n, 0, PASSES)

        def add_biases(t):
            for n in range(N_HALVES):
                add_bias(t, n)

        def load(t):
            if live(t):
                load_refs(t)
                if t % J == 0:
                    load_orig(t // J)

        max_of_halves(0)
        sum_gates(0, 1)
        on_vector(0, [0, 1])
        gate(TILES - 1)
        on_vector(0, [2])
        max_of_quarters(0)
        turn_orig(0)
        on_vector(0, [3])
        max_of_two(0)
        on_vector(0, [4, 5])
        copy_out_orig(0)
        on_scalar(0, [MAXIMUM, 6, 7])
        sum_gates(1, TILES)
        af_scale = spread_of_af()
        load(RAG_BUFS)

        max_of_halves(1)
        turn_orig(1)
        on_scalar(1, [0, 1])
        max_of_quarters(1)
        on_vector(1, [4])
        max_of_two(1)
        copy_out(0)
        on_vector(1, [5, 6, 7])
        on_scalar(1, [MAXIMUM])
        copy_out_orig(1)
        quantise_and_multiply(0)
        on_scalar(1, [2, 3])
        load(1 + RAG_BUFS)

        max_of_halves(2)
        on_scalar(2, [0, 1])
        turn_orig(2)
        nc.scalar.activation(out=first_table[:], in_=neg_half[:], func=ACT.Gelu)
        copy_out(1)
        max_of_quarters(2)
        add_biases(0)
        quantise_and_multiply(1)
        mean(0)
        on_scalar(2, [2])
        on_scalar(2, [3])
        on_vector(2, [6])
        on_vector(2, [7])
        max_of_two(2)
        variance(0)
        on_scalar(2, [MAXIMUM])
        add_biases(1)
        centre(0, whole)
        on_scalar(2, [4])
        copy_out_orig(2)
        mean(1)
        normalise(0, whole)
        on_scalar(2, [5])
        load(2 + RAG_BUFS)

        for step in range(3, TILES):
            pooling, multiplying, norming, ending = step, step - 1, step - 2, step - 3
            max_of_halves(pooling)
            on_scalar(pooling, [0])
            on_vector(pooling, [6])
            turn_orig(pooling)
            copy_out(multiplying)
            gelu(ending, whole)
            variance(norming)
            quantise_and_multiply(multiplying)
            max_of_quarters(pooling)
            residual(ending, whole)
            on_scalar(pooling, [1])
            on_scalar(pooling, [2])
            max_of_two(pooling)
            on_scalar(pooling, [3])
            add_biases(multiplying)
            on_gpsimd(pooling, [MAXIMUM])
            centre(norming, whole)
            on_scalar(pooling, [4])
            on_gpsimd(pooling, [7])
            copy_out_orig(pooling)
            normalise(norming, whole)
            mean(multiplying)
            on_scalar(pooling, [5])
            load(pooling + RAG_BUFS)

        ending, norming = last - 2, last - 1
        quantise(last, 0, HALF_PASSES)
        for n in range(N_HALVES):
            multiply(last, n, 0, HALF_PASSES)
        gelu(ending, whole)
        centre(norming, whole)
        copy_out_pooled(last, 0)
        copy_out_pooled(last, 1, True)
        for g in range(HALF_PASSES, PASSES):
            quantise(last, g, g + 1)
            for n in range(N_HALVES):
                multiply(last, n, g, g + 1)
        variance(norming)
        residual(ending, whole)
        add_biases(last)
        mean(last)
        square(last)
        for cols in halves:
            centre(last, cols)
        add_eps(last, nc.vector)
        invert_root(last)
        normalise(norming, whole)
        gelu(norming, whole)
        for cols in halves:
            normalise(last, cols)
            gelu(last, cols)
        residual(norming, whole)
        for cols in halves:
            residual(last, cols)
